import numpy as np
import ml_dtypes


def mxq(x, axis, fmt="e4m3"):
    dtype, down = {"e4m3": (ml_dtypes.float8_e4m3fn, 7), "e5m2": (ml_dtypes.float8_e5m2, 14)}[fmt]
    v = np.moveaxis(np.asarray(x, np.float32).astype(ml_dtypes.bfloat16).astype(np.float64), axis, -1)
    blocks = v.reshape(v.shape[:-1] + (-1, 32))
    amax = np.abs(blocks).max(-1, keepdims=True)
    byte = np.maximum(np.where(amax > 0, np.frexp(amax)[1] - 1 + 127, 0) - down, 1)
    scale = np.exp2(byte - 127.0)
    codes = (blocks / scale).astype(np.float32).astype(dtype).astype(np.float64)
    return np.moveaxis((codes * scale).reshape(v.shape), -1, axis)


WIDE = False


def mx_kscale(k):
    if not WIDE:
        return np.ones(k)
    levels = np.array([10, -10, 5, -5, 0])
    a = np.random.permutation(np.resize(levels, k // 512 * 4)).reshape(k // 512, 4)
    idx = np.arange(k)
    return np.exp2(a[idx // 512, idx % 128 // 32])


BF16 = ml_dtypes.bfloat16


def bf(x):
    return np.asarray(x, np.float32).astype(BF16)


def f64(x):
    return np.asarray(x).astype(np.float64)


E2M1 = np.array([0.0, 0.5, 1.0, 1.5, 2.0, 3.0, 4.0, 6.0, -0.0, -0.5, -1.0, -1.5, -2.0, -3.0, -4.0, -6.0])


def pack_weight(w, fmt):
    k, n = w.shape
    w = f64(bf(w)).reshape(k // 32, 32, n)
    amax = np.abs(w).max(1)
    if fmt == "e4m3":
        byte = np.frexp(amax)[1] - 1 + 127 - 7
    else:
        mant, ex = np.frexp(amax / 6.0)
        byte = np.where(mant > 0.5, ex, ex - 1) + 127
    byte = np.clip(np.where(amax > 0, byte, 1), 1, 254)
    scaled = (w * np.exp2(127.0 - byte)[:, None, :]).reshape(k, n).astype(np.float32)
    by_word = np.ascontiguousarray(scaled.reshape(k // 512, 128, 4, n).transpose(0, 1, 3, 2))
    if fmt == "e4m3":
        words = by_word.astype(ml_dtypes.float8_e4m3fn).view(np.uint8)
    else:
        c = by_word.astype(ml_dtypes.float4_e2m1fn).view(np.uint8) & 0xF
        words = c[..., 0::2] | (c[..., 1::2] << 4)
    return np.ascontiguousarray(words), np.ascontiguousarray(byte.astype(np.uint8).reshape(k // 512, 16, n))


def unpack_weight(words, scales, fmt):
    g, p, n, _ = words.shape
    if fmt == "e4m3":
        vals = np.ascontiguousarray(words).view(ml_dtypes.float8_e4m3fn).astype(np.float64)
    else:
        nib = np.empty((g, p, n, 4), np.uint8)
        nib[..., 0::2] = words & 0xF
        nib[..., 1::2] = words >> 4
        vals = E2M1[nib]
    vals = vals * np.repeat(np.exp2(scales.astype(np.float64) - 127.0), 8, axis=1)[..., None]
    return vals.transpose(0, 1, 3, 2).reshape(g * 512, n)

def pack4(w):
    words, scales = pack_weight(w, "e2m1")
    return words.reshape(words.shape[0], 128, -1), scales


def unpack4(words, scales):
    return unpack_weight(words.reshape(words.shape[0], 128, -1, 2), scales, "e2m1")


B, N, E, L, A, H1, H2, G = 1024, 8, 8, 512, 128, 1024, 512, 8


def mish(v):
    return v * np.tanh(np.log(1.0 + np.exp(v)))


def simnorm(v):
    vg = v.reshape(v.shape[:-1] + (v.shape[-1] // G, G))
    ex = np.exp(vg - vg.max(-1, keepdims=True))
    return (ex / ex.sum(-1, keepdims=True)).reshape(v.shape)


def setup_inputs():
    s = mx_kscale(H2)
    r = np.random.standard_normal
    h2 = bf(mish(r((B, E, H2))) * s)
    logits = bf(r((B, N, E)))
    stack = r((E, H2, L)) * 2.0 / np.sqrt(H2) / s[:, None]
    words, scales = pack4(stack.reshape(-1, L))
    b3 = bf(0.3 * r((E, L)))
    return {"h2": h2,
            "logits": logits,
            "W3_words": words,
            "W3_scales": scales,
            "b3": b3}


def reference(h2, logits, W3_words, W3_scales, b3):
    hq = mxq(f64(h2).transpose(1, 0, 2), 2, "e4m3")
    z = (hq @ unpack4(W3_words, W3_scales).reshape(E, H2, L)) + f64(b3)[:, None, :]
    y = simnorm(z)
    lg = f64(logits)
    ex = np.exp(lg - lg.max(-1, keepdims=True))
    comb = ex / ex.sum(-1, keepdims=True)
    return sum(comb[:, :, e, None] * y[e][:, None, :] for e in range(E))

@@ -1,0 +1,246 @@
+from contextlib import ExitStack
+
+import concourse.mybir as mybir
+from concourse.masks import make_identity
+
+F32 = mybir.dt.float32
+BF16 = mybir.dt.bfloat16
+I32 = mybir.dt.int32
+U32 = mybir.dt.uint32
+U8 = mybir.dt.uint8
+FP8X4 = mybir.dt.float8_e4m3fn_x4
+FP4X4 = mybir.dt.float4_e2m1fn_x4
+ALU = mybir.AluOpType
+ACT = mybir.ActivationFunctionType
+AXIS_X = mybir.AxisListType.X
+
+P = 128
+PACK = 4
+B, AGENTS, E, K, L = 1024, 8, 8, 512, 512
+GROUP = 8
+TILES = B // P
+WORDS = K // 2
+L_BLOCKS = L // P
+UNITS = 8
+ENTRIES = P // E
+TENSOR_TILES = 3
+
+FLOPS = 2 * B * E * K * L + 2 * B * AGENTS * E * L
+
+
+def combines_on_tensor(t):
+    return t % 2 == 1 and t // 2 < TENSOR_TILES
+
+
+def grouped_softmax(nc, small, dst, src, groups):
+    shape = [P, groups, GROUP]
+    src_g = src.rearrange("p (g j) -> p g j", j=GROUP)
+    dst_g = dst.rearrange("p (g j) -> p g j", j=GROUP)
+    top = small.tile([P, groups], F32, name="top")
+    nc.vector.tensor_reduce(out=top[:], in_=src_g, axis=AXIS_X, op=ALU.max)
+    nc.vector.tensor_tensor(
+        out=dst_g, in0=src_g, in1=top[:].unsqueeze(2).to_broadcast(shape), op=ALU.subtract
+    )
+    nc.scalar.activation(out=dst, in_=dst, func=ACT.Exp)
+    total = small.tile([P, groups], F32, name="total")
+    nc.vector.tensor_reduce(out=total[:], in_=dst_g, axis=AXIS_X, op=ALU.add)
+    nc.vector.reciprocal(out=total[:], in_=total[:])
+    nc.vector.tensor_tensor(
+        out=dst_g, in0=dst_g, in1=total[:].unsqueeze(2).to_broadcast(shape), op=ALU.mult
+    )
+
+
+def tile_softmoedynamics_pb_t_e_kernel(tc, h2, logits, W3_words, W3_scales, b3, out):
+    nc = tc.nc
+    out_rows = out.rearrange("b n l -> (b n) l")
+
+    with ExitStack() as ctx:
+        const = ctx.enter_context(tc.tile_pool(name="const", bufs=1))
+        x_pool = ctx.enter_context(tc.tile_pool(name="x", bufs=3))
+        quant = ctx.enter_context(tc.tile_pool(name="quant", bufs=2))
+        z_pool = ctx.enter_context(tc.tile_pool(name="z", bufs=2))
+        y_pool = ctx.enter_context(tc.tile_pool(name="y", bufs=4))
+        small = ctx.enter_context(tc.tile_pool(name="small", bufs=4))
+        acc_pool = ctx.enter_context(tc.tile_pool(name="acc", bufs=2))
+        psum = ctx.enter_context(tc.psum_pool(name="psum", bufs=2))
+
+        ident = const.tile([P, P], F32, name="ident")
+        make_identity(nc, ident[:])
+
+        w_words = const.tile([P, E, 2 * L], U8, align_bytes=64, name="w_words")
+        nc.sync.dma_start(
+            out=w_words[:].bitcast(I32), in_=W3_words.bitcast(I32).rearrange("e p n -> p e n")
+        )
+        w_scales = const.tile([P, E, L], U8, align_bytes=64, name="w_scales")
+        nc.vector.memset(w_scales[:].rearrange("p e n -> p (e n)").bitcast(I32), 0)
+        for quadrant in range(4):
+            nc.sync.dma_start(
+                out=w_scales[32 * quadrant : 32 * quadrant + 4].bitcast(I32),
+                in_=W3_scales.bitcast(I32)[:, 4 * quadrant : 4 * quadrant + 4, :].rearrange(
+                    "e r n -> r e n"
+                ),
+            )
+
+        bias_rows = const.tile([P, P], BF16, name="bias_rows")
+        nc.vector.memset(bias_rows[:], 0.0)
+        nc.sync.dma_start(
+            out=bias_rows[0 : E * L_BLOCKS, :], in_=b3.rearrange("e (c l) -> (e c) l", l=P)
+        )
+        bias_rows_f32 = const.tile([P, P], F32, name="bias_rows_f32")
+        nc.vector.tensor_copy(out=bias_rows_f32[:], in_=bias_rows[:])
+        bias_ps = psum.tile([P, P], F32, name="bias_ps", tag="o")
+        nc.tensor.transpose(bias_ps[:], bias_rows_f32[:], ident[:])
+        bias_cols = const.tile([P, P], F32, name="bias_cols")
+        nc.scalar.copy(out=bias_cols[:], in_=bias_ps[:])
+
+        logits_by_entry = const.tile([P, TILES * AGENTS * E], BF16, name="logits_by_entry")
+        nc.sync.dma_start(
+            out=logits_by_entry[:].rearrange("b (t c) -> b t c", t=TILES),
+            in_=logits.rearrange("(t b) n e -> b t (n e)", b=P),
+        )
+        comb = const.tile([P, TILES * AGENTS * E], F32, name="comb")
+        grouped_softmax(nc, small, comb[:], logits_by_entry[:], TILES * AGENTS)
+
+        mixes = TENSOR_TILES * UNITS
+        logits_by_agent = const.tile([P, mixes * E], BF16, name="logits_by_agent")
+        for t in range(TILES):
+            if combines_on_tensor(t):
+                first = (t // 2) * UNITS * E
+                nc.sync.dma_start(
+                    out=logits_by_agent[:, first : first + UNITS * E].rearrange(
+                        "r (g e) -> r g e", e=E
+                    ),
+                    in_=logits[t * P : (t + 1) * P].rearrange(
+                        "(g b) n e -> (b n) g e", b=ENTRIES
+                    ),
+                )
+        comb_by_agent = const.tile([P, mixes * E], F32, name="comb_by_agent")
+        grouped_softmax(nc, small, comb_by_agent[:], logits_by_agent[:], mixes)
+        own_entry = const.tile([P, ENTRIES], F32, name="own_entry")
+        nc.vector.tensor_reduce(
+            out=own_entry[:],
+            in_=ident[:].rearrange("p (b n) -> p b n", n=AGENTS),
+            axis=AXIS_X,
+            op=ALU.add,
+        )
+        spread = const.tile([P, mixes * E, ENTRIES], F32, name="spread")
+        spread_shape = [P, mixes * E, ENTRIES]
+        nc.vector.tensor_tensor(
+            out=spread[:],
+            in0=comb_by_agent[:].unsqueeze(2).to_broadcast(spread_shape),
+            in1=own_entry[:].unsqueeze(1).to_broadcast(spread_shape),
+            op=ALU.mult,
+        )
+        mix = const.tile([P, mixes, P], F32, name="mix")
+        for first in range(0, mixes, 4):
+            mix_ps = psum.tile([P, 4, P], F32, name="mix_ps", tag="o")
+            for i in range(4):
+                unit_rows = spread[:, (first + i) * E : (first + i + 1) * E, :]
+                nc.tensor.transpose(
+                    mix_ps[:, i, :], unit_rows.rearrange("p e b -> p (e b)"), ident[:]
+                )
+            nc.scalar.copy(out=mix[:, first : first + 4, :], in_=mix_ps[:])
+
+        for t in range(TILES):
+            on_tensor = combines_on_tensor(t)
+
+            x_sb = x_pool.tile([P, E * K], BF16, name="x_sb")
+            nc.sync.dma_start(
+                out=x_sb[:], in_=h2[t * P : (t + 1) * P].rearrange("b e k -> b (e k)")
+            )
+            x_words = x_sb[:].bitcast(F32)
+            grouped = quant.tile([P, E * P * PACK], BF16, align_bytes=64, name="grouped")
+            grouped_words = grouped[:].bitcast(F32).rearrange("p (e b u) -> p e b u", e=E, u=2)
+            for e in range(0, E, 2):
+                xt = psum.tile([P, 2, 2, P], F32, name="xt")
+                for i in range(2):
+                    for u in range(2):
+                        nc.tensor.transpose(
+                            xt[:, i, u, :],
+                            x_words[:, (e + i) * WORDS + u : (e + i + 1) * WORDS : 2],
+                            ident[:],
+                        )
+                nc.scalar.copy(
+                    out=grouped_words[:, e : e + 2], in_=xt[:].rearrange("p e u b -> p e b u")
+                )
+            codes = quant.tile([P, E * P], U32, align_bytes=64, name="codes")
+            h_scales = quant.tile([P, E * P], U8, align_bytes=64, name="h_scales")
+            nc.vector.quantize_mx(
+                out=codes[:].bitcast(FP8X4), scales=h_scales[:], in_=grouped[:]
+            )
+
+            zT_sb = z_pool.tile([P, L_BLOCKS, UNITS, P], F32, name="zT_sb")
+            for e in range(E):
+                batch = slice(e * P, (e + 1) * P)
+                zT = psum.tile([P, L_BLOCKS, P], F32, name="zT")
+                for c in range(L_BLOCKS):
+                    nc.tensor.matmul_mx(
+                        out=zT[:, c, :],
+                        lhsT=w_words[:, e, 2 * c * P : 2 * (c + 1) * P].bitcast(FP4X4),
+                        lhsT_scale=w_scales[:, e, c * P : (c + 1) * P],
+                        rhs=codes[:, batch].bitcast(FP8X4),
+                        rhs_scale=h_scales[:, batch],
+                        start=True,
+                        stop=True,
+                    )
+                for c in range(L_BLOCKS):
+                    if on_tensor:
+                        dst = zT_sb[:, c, :, e * ENTRIES : (e + 1) * ENTRIES]
+                        src = zT[:, c, :].rearrange("p (g b) -> p g b", b=ENTRIES)
+                    else:
+                        dst = zT_sb[:, c, e, :]
+                        src = zT[:, c, :]
+                    column = e * L_BLOCKS + c
+                    nc.scalar.activation(
+                        out=dst,
+                        in_=src,
+                        func=ACT.Identity,
+                        bias=bias_cols[:, column : column + 1],
+                        scale=1.0,
+                    )
+
+            if not on_tensor:
+                acc = acc_pool.tile([P, AGENTS, L], F32, name="acc")
+            for unit in range(UNITS):
+                z_ps = psum.tile([P, L], F32, name="z_ps")
+                for c in range(L_BLOCKS):
+                    nc.tensor.transpose(
+                        z_ps[:, c * P : (c + 1) * P], zT_sb[:, c, unit, :], ident[:]
+                    )
+                y = y_pool.tile([P, L], F32, name="y")
+                grouped_softmax(nc, small, y[:], z_ps[:], L // GROUP)
+
+                if on_tensor:
+                    o_ps = psum.tile([P, L], F32, name="o_ps", tag="o")
+                    nc.tensor.matmul(
+                        out=o_ps[:],
+                        lhsT=mix[:, (t // 2) * UNITS + unit, :],
+                        rhs=y[:],
+                        start=True,
+                        stop=True,
+                    )
+                    o_sb = y_pool.tile([P, L], F32, name="o_sb")
+                    nc.scalar.copy(out=o_sb[:], in_=o_ps[:])
+                    first_row = (t * P + unit * ENTRIES) * AGENTS
+                    nc.sync.dma_start(out=out_rows[first_row : first_row + P, :], in_=o_sb[:])
+                else:
+                    for n in range(AGENTS):
+                        column = (t * AGENTS + n) * E + unit
+                        weight = comb[:, column : column + 1]
+                        if unit == 0:
+                            nc.scalar.activation(
+                                out=acc[:, n, :], in_=y[:], func=ACT.Copy, scale=weight
+                            )
+                        else:
+                            nc.vector.scalar_tensor_tensor(
+                                out=acc[:, n, :],
+                                in0=y[:],
+                                scalar=weight,
+                                in1=acc[:, n, :],
+                                op0=ALU.mult,
+                                op1=ALU.add,
+                            )
+                        if unit == UNITS - 1:
+                            nc.sync.dma_start(
+                                out=out[t * P : (t + 1) * P, n, :], in_=acc[:, n, :]
+                            )

@@ -18,6 +18,7 @@ P = 128
 PACK = 4
 B, AGENTS, E, K, L = 1024, 8, 8, 512, 512
 GROUP = 8
+GROUPS = L // GROUP
 TILES = B // P
 WORDS = K // 2
 L_BLOCKS = L // P
@@ -27,27 +28,35 @@ TENSOR_TILES = 3
 
 FLOPS = 2 * B * E * K * L + 2 * B * AGENTS * E * L
 
+TOTAL_UNITS = TILES * UNITS
+PAIRS = E // 2
+
+STORE = -1
+COMBINE = 0
+NORMALISE = COMBINE + 1
+INVERT = NORMALISE + 2
+ADD_UP = INVERT + UNITS
+EXPONENT = ADD_UP + 1
+SHIFT = EXPONENT + 1
+TURN_BACK = SHIFT + 1
+ADD_BIAS = TURN_BACK + UNITS
+MULTIPLY = ADD_BIAS + 1
+QUANTISE = MULTIPLY + 1
+REGROUP = QUANTISE + PAIRS
+TURN_H2 = REGROUP + 1
+LOAD = TURN_H2 + UNITS
+
 
 def combines_on_tensor(t):
     return t % 2 == 1 and t // 2 < TENSOR_TILES
 
 
-def grouped_softmax(nc, small, dst, src, groups):
-    shape = [P, groups, GROUP]
-    src_g = src.rearrange("p (g j) -> p g j", j=GROUP)
-    dst_g = dst.rearrange("p (g j) -> p g j", j=GROUP)
-    top = small.tile([P, groups], F32, name="top")
-    nc.vector.tensor_reduce(out=top[:], in_=src_g, axis=AXIS_X, op=ALU.max)
-    nc.vector.tensor_tensor(
-        out=dst_g, in0=src_g, in1=top[:].unsqueeze(2).to_broadcast(shape), op=ALU.subtract
-    )
-    nc.scalar.activation(out=dst, in_=dst, func=ACT.Exp)
-    total = small.tile([P, groups], F32, name="total")
-    nc.vector.tensor_reduce(out=total[:], in_=dst_g, axis=AXIS_X, op=ALU.add)
-    nc.vector.reciprocal(out=total[:], in_=total[:])
-    nc.vector.tensor_tensor(
-        out=dst_g, in0=dst_g, in1=total[:].unsqueeze(2).to_broadcast(shape), op=ALU.mult
-    )
+def by_group(ap):
+    return ap.rearrange("p (g j) -> p g j", j=GROUP)
+
+
+def over_group(ap, groups):
+    return ap.unsqueeze(2).to_broadcast([P, groups, GROUP])
 
 
 def tile_softmoedynamics_pb_t_e_kernel(tc, h2, logits, W3_words, W3_scales, b3, out):
@@ -56,11 +65,13 @@ def tile_softmoedynamics_pb_t_e_kernel(tc, h2, logits, W3_words, W3_scales, b3, 
 
     with ExitStack() as ctx:
         const = ctx.enter_context(tc.tile_pool(name="const", bufs=1))
-        x_pool = ctx.enter_context(tc.tile_pool(name="x", bufs=3))
+        x_pool = ctx.enter_context(tc.tile_pool(name="x", bufs=2))
         quant = ctx.enter_context(tc.tile_pool(name="quant", bufs=2))
         z_pool = ctx.enter_context(tc.tile_pool(name="z", bufs=2))
-        y_pool = ctx.enter_context(tc.tile_pool(name="y", bufs=4))
-        small = ctx.enter_context(tc.tile_pool(name="small", bufs=4))
+        y_pool = ctx.enter_context(tc.tile_pool(name="y", bufs=SHIFT + 2))
+        f_pool = ctx.enter_context(tc.tile_pool(name="f", bufs=3))
+        o_pool = ctx.enter_context(tc.tile_pool(name="o", bufs=3))
+        small = ctx.enter_context(tc.tile_pool(name="small", bufs=2))
         acc_pool = ctx.enter_context(tc.tile_pool(name="acc", bufs=2))
         psum = ctx.enter_context(tc.psum_pool(name="psum", bufs=2))
 
@@ -88,34 +99,49 @@ def tile_softmoedynamics_pb_t_e_kernel(tc, h2, logits, W3_words, W3_scales, b3, 
         )
         bias_rows_f32 = const.tile([P, P], F32, name="bias_rows_f32")
         nc.vector.tensor_copy(out=bias_rows_f32[:], in_=bias_rows[:])
-        bias_ps = psum.tile([P, P], F32, name="bias_ps", tag="o")
+        bias_ps = psum.tile([P, P], F32, name="bias_ps", tag="o_ps")
         nc.tensor.transpose(bias_ps[:], bias_rows_f32[:], ident[:])
         bias_cols = const.tile([P, P], F32, name="bias_cols")
         nc.scalar.copy(out=bias_cols[:], in_=bias_ps[:])
 
-        logits_by_entry = const.tile([P, TILES * AGENTS * E], BF16, name="logits_by_entry")
+        rows_by_entry = TILES * AGENTS
+        mixes = TENSOR_TILES * UNITS
+        rows = rows_by_entry + mixes
+        raw = const.tile([P, rows * E], BF16, name="raw")
         nc.sync.dma_start(
-            out=logits_by_entry[:].rearrange("b (t c) -> b t c", t=TILES),
+            out=raw[:, 0 : rows_by_entry * E].rearrange("b (t c) -> b t c", t=TILES),
             in_=logits.rearrange("(t b) n e -> b t (n e)", b=P),
         )
-        comb = const.tile([P, TILES * AGENTS * E], F32, name="comb")
-        grouped_softmax(nc, small, comb[:], logits_by_entry[:], TILES * AGENTS)
-
-        mixes = TENSOR_TILES * UNITS
-        logits_by_agent = const.tile([P, mixes * E], BF16, name="logits_by_agent")
         for t in range(TILES):
             if combines_on_tensor(t):
-                first = (t // 2) * UNITS * E
+                first = (rows_by_entry + (t // 2) * UNITS) * E
                 nc.sync.dma_start(
-                    out=logits_by_agent[:, first : first + UNITS * E].rearrange(
-                        "r (g e) -> r g e", e=E
-                    ),
+                    out=raw[:, first : first + UNITS * E].rearrange("r (g e) -> r g e", e=E),
                     in_=logits[t * P : (t + 1) * P].rearrange(
                         "(g b) n e -> (b n) g e", b=ENTRIES
                     ),
                 )
-        comb_by_agent = const.tile([P, mixes * E], F32, name="comb_by_agent")
-        grouped_softmax(nc, small, comb_by_agent[:], logits_by_agent[:], mixes)
+        comb = const.tile([P, rows * E], F32, name="comb")
+        comb_top = const.tile([P, rows], F32, name="comb_top")
+        comb_sum = const.tile([P, rows], F32, name="comb_sum")
+        nc.vector.tensor_reduce(out=comb_top[:], in_=by_group(raw[:]), axis=AXIS_X, op=ALU.max)
+        nc.vector.tensor_tensor(
+            out=by_group(comb[:]),
+            in0=by_group(raw[:]),
+            in1=over_group(comb_top[:], rows),
+            op=ALU.subtract,
+        )
+        nc.scalar.activation(out=comb[:], in_=comb[:], func=ACT.Exp)
+        nc.vector.tensor_reduce(out=comb_sum[:], in_=by_group(comb[:]), axis=AXIS_X, op=ALU.add)
+        nc.vector.reciprocal(out=comb_sum[:], in_=comb_sum[:])
+        nc.vector.tensor_tensor(
+            out=by_group(comb[:]),
+            in0=by_group(comb[:]),
+            in1=over_group(comb_sum[:], rows),
+            op=ALU.mult,
+        )
+        comb_by_agent = comb[:, rows_by_entry * E :]
+
         own_entry = const.tile([P, ENTRIES], F32, name="own_entry")
         nc.vector.tensor_reduce(
             out=own_entry[:],
@@ -127,13 +153,13 @@ def tile_softmoedynamics_pb_t_e_kernel(tc, h2, logits, W3_words, W3_scales, b3, 
         spread_shape = [P, mixes * E, ENTRIES]
         nc.vector.tensor_tensor(
             out=spread[:],
-            in0=comb_by_agent[:].unsqueeze(2).to_broadcast(spread_shape),
+            in0=comb_by_agent.unsqueeze(2).to_broadcast(spread_shape),
             in1=own_entry[:].unsqueeze(1).to_broadcast(spread_shape),
             op=ALU.mult,
         )
         mix = const.tile([P, mixes, P], F32, name="mix")
         for first in range(0, mixes, 4):
-            mix_ps = psum.tile([P, 4, P], F32, name="mix_ps", tag="o")
+            mix_ps = psum.tile([P, 4, P], F32, name="mix_ps", tag="o_ps")
             for i in range(4):
                 unit_rows = spread[:, (first + i) * E : (first + i + 1) * E, :]
                 nc.tensor.transpose(
@@ -141,106 +167,227 @@ def tile_softmoedynamics_pb_t_e_kernel(tc, h2, logits, W3_words, W3_scales, b3, 
                 )
             nc.scalar.copy(out=mix[:, first : first + 4, :], in_=mix_ps[:])
 
-        for t in range(TILES):
-            on_tensor = combines_on_tensor(t)
+        x_of, grouped_of, codes_of, h_scales_of, zT_sb_of, factors_of, acc_of = (
+            {}, {}, {}, {}, {}, {}, {},
+        )
+        xt_of, zT_of, z_ps_of, top_of, y_of, o_ps_of = {}, {}, {}, {}, {}, {}
 
+        def load(t):
             x_sb = x_pool.tile([P, E * K], BF16, name="x_sb")
             nc.sync.dma_start(
                 out=x_sb[:], in_=h2[t * P : (t + 1) * P].rearrange("b e k -> b (e k)")
             )
-            x_words = x_sb[:].bitcast(F32)
-            grouped = quant.tile([P, E * P * PACK], BF16, align_bytes=64, name="grouped")
-            grouped_words = grouped[:].bitcast(F32).rearrange("p (e b u) -> p e b u", e=E, u=2)
-            for e in range(0, E, 2):
-                xt = psum.tile([P, 2, 2, P], F32, name="xt")
-                for i in range(2):
-                    for u in range(2):
-                        nc.tensor.transpose(
-                            xt[:, i, u, :],
-                            x_words[:, (e + i) * WORDS + u : (e + i + 1) * WORDS : 2],
-                            ident[:],
-                        )
-                nc.scalar.copy(
-                    out=grouped_words[:, e : e + 2], in_=xt[:].rearrange("p e u b -> p e b u")
-                )
+            x_of[t] = x_sb
+
+        def turn_h2(t, pair):
+            x_words = x_of[t][:].bitcast(F32)
+            xt = psum.tile([P, 2, 2, P], F32, name="xt")
+            for i in range(2):
+                e = 2 * pair + i
+                for u in range(2):
+                    nc.tensor.transpose(
+                        xt[:, i, u, :], x_words[:, e * WORDS + u : (e + 1) * WORDS : 2], ident[:]
+                    )
+            xt_of[t, pair] = xt
+
+        def regroup(t, pair):
+            if pair == 0:
+                grouped = quant.tile([P, E * P * PACK], BF16, align_bytes=64, name="grouped")
+                grouped_of[t] = grouped
+            words = grouped_of[t][:].bitcast(F32).rearrange("p (e b u) -> p e b u", e=E, u=2)
+            nc.scalar.copy(
+                out=words[:, 2 * pair : 2 * pair + 2],
+                in_=xt_of[t, pair][:].rearrange("p e u b -> p e b u"),
+            )
+
+        def quantise(t):
             codes = quant.tile([P, E * P], U32, align_bytes=64, name="codes")
             h_scales = quant.tile([P, E * P], U8, align_bytes=64, name="h_scales")
             nc.vector.quantize_mx(
-                out=codes[:].bitcast(FP8X4), scales=h_scales[:], in_=grouped[:]
+                out=codes[:].bitcast(FP8X4), scales=h_scales[:], in_=grouped_of[t][:]
+            )
+            codes_of[t] = codes
+            h_scales_of[t] = h_scales
+
+        def multiply(t, e):
+            batch = slice(e * P, (e + 1) * P)
+            zT = psum.tile([P, L_BLOCKS, P], F32, name="zT")
+            for c in range(L_BLOCKS):
+                nc.tensor.matmul_mx(
+                    out=zT[:, c, :],
+                    lhsT=w_words[:, e, 2 * c * P : 2 * (c + 1) * P].bitcast(FP4X4),
+                    lhsT_scale=w_scales[:, e, c * P : (c + 1) * P],
+                    rhs=codes_of[t][:, batch].bitcast(FP8X4),
+                    rhs_scale=h_scales_of[t][:, batch],
+                    start=True,
+                    stop=True,
+                )
+            zT_of[t, e] = zT
+
+        def add_bias(t, e):
+            if e == 0:
+                zT_sb = z_pool.tile([P, L_BLOCKS, UNITS, P], F32, name="zT_sb")
+                zT_sb_of[t] = zT_sb
+            for c in range(L_BLOCKS):
+                if combines_on_tensor(t):
+                    dst = zT_sb_of[t][:, c, :, e * ENTRIES : (e + 1) * ENTRIES]
+                    src = zT_of[t, e][:, c, :].rearrange("p (g b) -> p g b", b=ENTRIES)
+                else:
+                    dst = zT_sb_of[t][:, c, e, :]
+                    src = zT_of[t, e][:, c, :]
+                column = e * L_BLOCKS + c
+                nc.scalar.activation(
+                    out=dst,
+                    in_=src,
+                    func=ACT.Identity,
+                    bias=bias_cols[:, column : column + 1],
+                    scale=1.0,
+                )
+
+        def turn_back(t, unit):
+            z_ps = psum.tile([P, L], F32, name="z_ps")
+            for c in range(L_BLOCKS):
+                nc.tensor.transpose(
+                    z_ps[:, c * P : (c + 1) * P], zT_sb_of[t][:, c, unit, :], ident[:]
+                )
+            z_ps_of[t, unit] = z_ps
+
+        def find_top(t, unit):
+            top = small.tile([P, GROUPS], F32, name="top")
+            nc.vector.tensor_reduce(
+                out=top[:], in_=by_group(z_ps_of[t, unit][:]), axis=AXIS_X, op=ALU.max
+            )
+            top_of[t, unit] = top
+
+        def shift(t, unit):
+            y = y_pool.tile([P, L], F32, name="y")
+            nc.vector.tensor_tensor(
+                out=by_group(y[:]),
+                in0=by_group(z_ps_of[t, unit][:]),
+                in1=over_group(top_of[t, unit][:], GROUPS),
+                op=ALU.subtract,
+            )
+            y_of[t, unit] = y
+
+        def exponent(t, unit):
+            nc.scalar.activation(out=y_of[t, unit][:], in_=y_of[t, unit][:], func=ACT.Exp)
+
+        def add_up(t, unit):
+            if unit == 0:
+                factors = f_pool.tile([P, UNITS, GROUPS], F32, name="factors")
+                factors_of[t] = factors
+            nc.vector.tensor_reduce(
+                out=factors_of[t][:, unit, :],
+                in_=by_group(y_of[t, unit][:]),
+                axis=AXIS_X,
+                op=ALU.add,
             )
 
-            zT_sb = z_pool.tile([P, L_BLOCKS, UNITS, P], F32, name="zT_sb")
-            for e in range(E):
-                batch = slice(e * P, (e + 1) * P)
-                zT = psum.tile([P, L_BLOCKS, P], F32, name="zT")
-                for c in range(L_BLOCKS):
-                    nc.tensor.matmul_mx(
-                        out=zT[:, c, :],
-                        lhsT=w_words[:, e, 2 * c * P : 2 * (c + 1) * P].bitcast(FP4X4),
-                        lhsT_scale=w_scales[:, e, c * P : (c + 1) * P],
-                        rhs=codes[:, batch].bitcast(FP8X4),
-                        rhs_scale=h_scales[:, batch],
-                        start=True,
-                        stop=True,
-                    )
-                for c in range(L_BLOCKS):
-                    if on_tensor:
-                        dst = zT_sb[:, c, :, e * ENTRIES : (e + 1) * ENTRIES]
-                        src = zT[:, c, :].rearrange("p (g b) -> p g b", b=ENTRIES)
-                    else:
-                        dst = zT_sb[:, c, e, :]
-                        src = zT[:, c, :]
-                    column = e * L_BLOCKS + c
-                    nc.scalar.activation(
-                        out=dst,
-                        in_=src,
-                        func=ACT.Identity,
-                        bias=bias_cols[:, column : column + 1],
-                        scale=1.0,
-                    )
+        def invert(t):
+            sums = factors_of[t][:].rearrange("p u g -> p (u g)")
+            nc.scalar.activation(out=sums, in_=sums, func=ACT.Ln)
+            nc.scalar.activation(out=sums, in_=sums, func=ACT.Exp, scale=-1.0)
 
-            if not on_tensor:
+        def normalise(t, unit):
+            nc.vector.tensor_tensor(
+                out=by_group(y_of[t, unit][:]),
+                in0=by_group(y_of[t, unit][:]),
+                in1=over_group(factors_of[t][:, unit, :], GROUPS),
+                op=ALU.mult,
+            )
+
+        def combine_on_tensor(t, unit):
+            o_ps = psum.tile([P, L], F32, name="o_ps")
+            nc.tensor.matmul(
+                out=o_ps[:],
+                lhsT=mix[:, (t // 2) * UNITS + unit, :],
+                rhs=y_of[t, unit][:],
+                start=True,
+                stop=True,
+            )
+            o_ps_of[t, unit] = o_ps
+
+        def store_from_tensor(t, unit):
+            o_sb = o_pool.tile([P, L], F32, name="o_sb")
+            nc.scalar.copy(out=o_sb[:], in_=o_ps_of[t, unit][:])
+            first_row = (t * P + unit * ENTRIES) * AGENTS
+            nc.sync.dma_start(out=out_rows[first_row : first_row + P, :], in_=o_sb[:])
+
+        def combine_on_vector(t, e):
+            if e == 0:
                 acc = acc_pool.tile([P, AGENTS, L], F32, name="acc")
-            for unit in range(UNITS):
-                z_ps = psum.tile([P, L], F32, name="z_ps")
-                for c in range(L_BLOCKS):
-                    nc.tensor.transpose(
-                        z_ps[:, c * P : (c + 1) * P], zT_sb[:, c, unit, :], ident[:]
-                    )
-                y = y_pool.tile([P, L], F32, name="y")
-                grouped_softmax(nc, small, y[:], z_ps[:], L // GROUP)
-
-                if on_tensor:
-                    o_ps = psum.tile([P, L], F32, name="o_ps", tag="o")
-                    nc.tensor.matmul(
-                        out=o_ps[:],
-                        lhsT=mix[:, (t // 2) * UNITS + unit, :],
-                        rhs=y[:],
-                        start=True,
-                        stop=True,
-                    )
-                    o_sb = y_pool.tile([P, L], F32, name="o_sb")
-                    nc.scalar.copy(out=o_sb[:], in_=o_ps[:])
-                    first_row = (t * P + unit * ENTRIES) * AGENTS
-                    nc.sync.dma_start(out=out_rows[first_row : first_row + P, :], in_=o_sb[:])
+                acc_of[t] = acc
+            for n in range(AGENTS):
+                column = (t * AGENTS + n) * E + e
+                weight = comb[:, column : column + 1]
+                term = acc_of[t][:, n, :]
+                if e == 0:
+                    nc.scalar.activation(out=term, in_=y_of[t, e][:], func=ACT.Copy, scale=weight)
                 else:
-                    for n in range(AGENTS):
-                        column = (t * AGENTS + n) * E + unit
-                        weight = comb[:, column : column + 1]
-                        if unit == 0:
-                            nc.scalar.activation(
-                                out=acc[:, n, :], in_=y[:], func=ACT.Copy, scale=weight
-                            )
-                        else:
-                            nc.vector.scalar_tensor_tensor(
-                                out=acc[:, n, :],
-                                in0=y[:],
-                                scalar=weight,
-                                in1=acc[:, n, :],
-                                op0=ALU.mult,
-                                op1=ALU.add,
-                            )
-                        if unit == UNITS - 1:
-                            nc.sync.dma_start(
-                                out=out[t * P : (t + 1) * P, n, :], in_=acc[:, n, :]
-                            )
+                    nc.vector.scalar_tensor_tensor(
+                        out=term,
+                        in0=y_of[t, e][:],
+                        scalar=weight,
+                        in1=term,
+                        op0=ALU.mult,
+                        op1=ALU.add,
+                    )
+                if e == E - 1:
+                    nc.sync.dma_start(out=out[t * P : (t + 1) * P, n, :], in_=term)
+
+        def at(step, ahead):
+            return divmod(step + ahead, UNITS)
+
+        def real(t):
+            return 0 <= t < TILES
+
+        with tc.manual_schedule():
+            for step in range(-LOAD, TOTAL_UNITS - STORE):
+                t, unit = at(step, EXPONENT)
+                if real(t):
+                    exponent(t, unit)
+                t, unit = at(step, INVERT)
+                if real(t) and unit == 0:
+                    invert(t)
+                t, unit = at(step, SHIFT)
+                if real(t):
+                    find_top(t, unit)
+                t, unit = at(step, ADD_UP)
+                if real(t):
+                    add_up(t, unit)
+                t, unit = at(step, SHIFT)
+                if real(t):
+                    shift(t, unit)
+                t, unit = at(step, NORMALISE)
+                if real(t):
+                    normalise(t, unit)
+                t, unit = at(step, QUANTISE)
+                if real(t) and unit == 0:
+                    quantise(t)
+                t, unit = at(step, COMBINE)
+                if real(t):
+                    if combines_on_tensor(t):
+                        combine_on_tensor(t, unit)
+                    else:
+                        combine_on_vector(t, unit)
+                t, unit = at(step, STORE)
+                if real(t) and combines_on_tensor(t):
+                    store_from_tensor(t, unit)
+                t, unit = at(step, TURN_BACK)
+                if real(t):
+                    turn_back(t, unit)
+                t, unit = at(step, ADD_BIAS)
+                if real(t):
+                    add_bias(t, unit)
+                t, unit = at(step, MULTIPLY)
+                if real(t):
+                    multiply(t, unit)
+                t, unit = at(step, REGROUP)
+                if real(t) and unit < PAIRS:
+                    regroup(t, unit)
+                t, unit = at(step, TURN_H2)
+                if real(t) and unit < PAIRS:
+                    turn_h2(t, unit)
+                t, unit = at(step, LOAD)
+                if real(t) and unit == 0:
+                    load(t)

@@ -289,7 +289,7 @@ def tile_softmoedynamics_pb_t_e_kernel(tc, h2, logits, W3_words, W3_scales, b3, 
             nc.scalar.activation(out=sums, in_=sums, func=ACT.Exp, scale=-1.0)
 
         def normalise(t, unit):
-            nc.vector.tensor_tensor(
+            nc.gpsimd.tensor_tensor(
                 out=by_group(y_of[t, unit][:]),
                 in0=by_group(y_of[t, unit][:]),
                 in1=over_group(factors_of[t][:, unit, :], GROUPS),

@@ -69,6 +69,7 @@ def tile_softmoedynamics_pb_t_e_kernel(tc, h2, logits, W3_words, W3_scales, b3, 
         quant = ctx.enter_context(tc.tile_pool(name="quant", bufs=2))
         z_pool = ctx.enter_context(tc.tile_pool(name="z", bufs=2))
         y_pool = ctx.enter_context(tc.tile_pool(name="y", bufs=SHIFT + 2))
+        yn_pool = ctx.enter_context(tc.tile_pool(name="yn", bufs=2))
         f_pool = ctx.enter_context(tc.tile_pool(name="f", bufs=3))
         o_pool = ctx.enter_context(tc.tile_pool(name="o", bufs=3))
         small = ctx.enter_context(tc.tile_pool(name="small", bufs=2))
@@ -170,7 +171,7 @@ def tile_softmoedynamics_pb_t_e_kernel(tc, h2, logits, W3_words, W3_scales, b3, 
         x_of, grouped_of, codes_of, h_scales_of, zT_sb_of, factors_of, acc_of = (
             {}, {}, {}, {}, {}, {}, {},
         )
-        xt_of, zT_of, z_ps_of, top_of, y_of, o_ps_of = {}, {}, {}, {}, {}, {}
+        xt_of, zT_of, z_ps_of, top_of, y_of, o_ps_of, yn_of = {}, {}, {}, {}, {}, {}, {}
 
         def load(t):
             x_sb = x_pool.tile([P, E * K], BF16, name="x_sb")
@@ -289,8 +290,10 @@ def tile_softmoedynamics_pb_t_e_kernel(tc, h2, logits, W3_words, W3_scales, b3, 
             nc.scalar.activation(out=sums, in_=sums, func=ACT.Exp, scale=-1.0)
 
         def normalise(t, unit):
+            yn = yn_pool.tile([P, L], F32, name="yn")
+            yn_of[t, unit] = yn
             nc.gpsimd.tensor_tensor(
-                out=by_group(y_of[t, unit][:]),
+                out=by_group(yn[:]),
                 in0=by_group(y_of[t, unit][:]),
                 in1=over_group(factors_of[t][:, unit, :], GROUPS),
                 op=ALU.mult,
@@ -301,7 +304,7 @@ def tile_softmoedynamics_pb_t_e_kernel(tc, h2, logits, W3_words, W3_scales, b3, 
             nc.tensor.matmul(
                 out=o_ps[:],
                 lhsT=mix[:, (t // 2) * UNITS + unit, :],
-                rhs=y_of[t, unit][:],
+                rhs=yn_of[t, unit][:],
                 start=True,
                 stop=True,
             )
@@ -322,11 +325,11 @@ def tile_softmoedynamics_pb_t_e_kernel(tc, h2, logits, W3_words, W3_scales, b3, 
                 weight = comb[:, column : column + 1]
                 term = acc_of[t][:, n, :]
                 if e == 0:
-                    nc.scalar.activation(out=term, in_=y_of[t, e][:], func=ACT.Copy, scale=weight)
+                    nc.scalar.activation(out=term, in_=yn_of[t, e][:], func=ACT.Copy, scale=weight)
                 else:
                     nc.vector.scalar_tensor_tensor(
                         out=term,
-                        in0=y_of[t, e][:],
+                        in0=yn_of[t, e][:],
                         scalar=weight,
                         in1=term,
                         op0=ALU.mult,

@@ -101,7 +101,14 @@ def tile_softmoedynamics_pb_t_e_kernel(tc, h2, logits, W3_words, W3_scales, b3, 
         bias_rows_f32 = const.tile([P, P], F32, name="bias_rows_f32")
         nc.vector.tensor_copy(out=bias_rows_f32[:], in_=bias_rows[:])
         bias_ps = psum.tile([P, P], F32, name="bias_ps", tag="o_ps")
-        nc.tensor.transpose(bias_ps[:], bias_rows_f32[:], ident[:])
+        zero_rows = const.tile([P, P], F32, name="zero_rows")
+        nc.vector.memset(zero_rows[:], 0.0)
+        nc.tensor.matmul(
+            out=bias_ps[:], lhsT=bias_rows_f32[:], rhs=ident[:], is_transpose=True, start=True, stop=False
+        )
+        nc.tensor.matmul(
+            out=bias_ps[:], lhsT=zero_rows[:], rhs=ident[:], is_transpose=True, start=False, stop=True
+        )
         bias_cols = const.tile([P, P], F32, name="bias_cols")
         nc.scalar.copy(out=bias_cols[:], in_=bias_ps[:])
 

@@ -25,24 +25,27 @@ L_BLOCKS = L // P
 UNITS = 8
 ENTRIES = P // E
 TENSOR_TILES = 3
+SCALAR_TERMS = 3
 
 FLOPS = 2 * B * E * K * L + 2 * B * AGENTS * E * L
 
 TOTAL_UNITS = TILES * UNITS
 PAIRS = E // 2
 
-STORE = -1
+STORE = -3
+TURN_OUT = -2
+LIFT = -1
 COMBINE = 0
-NORMALISE = COMBINE + 1
-INVERT = NORMALISE + 2
-ADD_UP = INVERT + UNITS
+WEIGH = COMBINE + 1
+NORMALISE = WEIGH + UNITS + 1
+ADD_UP = NORMALISE
 EXPONENT = ADD_UP + 1
 SHIFT = EXPONENT + 1
 TURN_BACK = SHIFT + 1
 ADD_BIAS = TURN_BACK + UNITS
 MULTIPLY = ADD_BIAS + 1
 QUANTISE = MULTIPLY + 1
-REGROUP = QUANTISE + PAIRS
+REGROUP = QUANTISE + 1
 TURN_H2 = REGROUP + 1
 LOAD = TURN_H2 + UNITS
 
@@ -68,16 +71,17 @@ def tile_softmoedynamics_pb_t_e_kernel(tc, h2, logits, W3_words, W3_scales, b3, 
         x_pool = ctx.enter_context(tc.tile_pool(name="x", bufs=2))
         quant = ctx.enter_context(tc.tile_pool(name="quant", bufs=2))
         z_pool = ctx.enter_context(tc.tile_pool(name="z", bufs=2))
-        y_pool = ctx.enter_context(tc.tile_pool(name="y", bufs=SHIFT + 2))
-        yn_pool = ctx.enter_context(tc.tile_pool(name="yn", bufs=2))
-        f_pool = ctx.enter_context(tc.tile_pool(name="f", bufs=3))
+        y_pool = ctx.enter_context(tc.tile_pool(name="y", bufs=SHIFT + UNITS))
+        term_pool = ctx.enter_context(tc.tile_pool(name="term", bufs=2 * E))
         o_pool = ctx.enter_context(tc.tile_pool(name="o", bufs=3))
-        small = ctx.enter_context(tc.tile_pool(name="small", bufs=2))
-        acc_pool = ctx.enter_context(tc.tile_pool(name="acc", bufs=2))
+        small = ctx.enter_context(tc.tile_pool(name="small", bufs=3))
+        psum_one = ctx.enter_context(tc.psum_pool(name="psum_one", bufs=1))
         psum = ctx.enter_context(tc.psum_pool(name="psum", bufs=2))
 
         ident = const.tile([P, P], F32, name="ident")
         make_identity(nc, ident[:])
+        minus_one = const.tile([P, GROUPS], F32, name="minus_one")
+        nc.vector.memset(minus_one[:], -1.0)
 
         w_words = const.tile([P, E, 2 * L], U8, align_bytes=64, name="w_words")
         nc.sync.dma_start(
@@ -101,14 +105,7 @@ def tile_softmoedynamics_pb_t_e_kernel(tc, h2, logits, W3_words, W3_scales, b3, 
         bias_rows_f32 = const.tile([P, P], F32, name="bias_rows_f32")
         nc.vector.tensor_copy(out=bias_rows_f32[:], in_=bias_rows[:])
         bias_ps = psum.tile([P, P], F32, name="bias_ps", tag="o_ps")
-        zero_rows = const.tile([P, P], F32, name="zero_rows")
-        nc.vector.memset(zero_rows[:], 0.0)
-        nc.tensor.matmul(
-            out=bias_ps[:], lhsT=bias_rows_f32[:], rhs=ident[:], is_transpose=True, start=True, stop=False
-        )
-        nc.tensor.matmul(
-            out=bias_ps[:], lhsT=zero_rows[:], rhs=ident[:], is_transpose=True, start=False, stop=True
-        )
+        nc.tensor.transpose(bias_ps[:], bias_rows_f32[:], ident[:])
         bias_cols = const.tile([P, P], F32, name="bias_cols")
         nc.scalar.copy(out=bias_cols[:], in_=bias_ps[:])
 
@@ -175,10 +172,9 @@ def tile_softmoedynamics_pb_t_e_kernel(tc, h2, logits, W3_words, W3_scales, b3, 
                 )
             nc.scalar.copy(out=mix[:, first : first + 4, :], in_=mix_ps[:])
 
-        x_of, grouped_of, codes_of, h_scales_of, zT_sb_of, factors_of, acc_of = (
-            {}, {}, {}, {}, {}, {}, {},
-        )
-        xt_of, zT_of, z_ps_of, top_of, y_of, o_ps_of, yn_of = {}, {}, {}, {}, {}, {}, {}
+        x_of, grouped_of, codes_of, h_scales_of, zT_sb_of = {}, {}, {}, {}, {}
+        xt_of, zT_of, z_ps_of, top_of, y_of, total_of, o_ps_of = {}, {}, {}, {}, {}, {}, {}
+        terms_of, sumT_of, sumT_sb_of = {}, {}, {}
 
         def load(t):
             x_sb = x_pool.tile([P, E * K], BF16, name="x_sb")
@@ -189,7 +185,7 @@ def tile_softmoedynamics_pb_t_e_kernel(tc, h2, logits, W3_words, W3_scales, b3, 
 
         def turn_h2(t, pair):
             x_words = x_of[t][:].bitcast(F32)
-            xt = psum.tile([P, 2, 2, P], F32, name="xt")
+            xt = psum_one.tile([P, 2, 2, P], F32, name="xt")
             for i in range(2):
                 e = 2 * pair + i
                 for u in range(2):
@@ -208,18 +204,22 @@ def tile_softmoedynamics_pb_t_e_kernel(tc, h2, logits, W3_words, W3_scales, b3, 
                 in_=xt_of[t, pair][:].rearrange("p e u b -> p e b u"),
             )
 
-        def quantise(t):
-            codes = quant.tile([P, E * P], U32, align_bytes=64, name="codes")
-            h_scales = quant.tile([P, E * P], U8, align_bytes=64, name="h_scales")
+        def quantise(t, pair):
+            if pair == 0:
+                codes = quant.tile([P, E * P], U32, align_bytes=64, name="codes")
+                h_scales = quant.tile([P, E * P], U8, align_bytes=64, name="h_scales")
+                codes_of[t] = codes
+                h_scales_of[t] = h_scales
+            columns = slice(2 * pair * P, 2 * (pair + 1) * P)
             nc.vector.quantize_mx(
-                out=codes[:].bitcast(FP8X4), scales=h_scales[:], in_=grouped_of[t][:]
+                out=codes_of[t][:, columns].bitcast(FP8X4),
+                scales=h_scales_of[t][:, columns],
+                in_=grouped_of[t][:, 2 * pair * P * PACK : 2 * (pair + 1) * P * PACK],
             )
-            codes_of[t] = codes
-            h_scales_of[t] = h_scales
 
         def multiply(t, e):
             batch = slice(e * P, (e + 1) * P)
-            zT = psum.tile([P, L_BLOCKS, P], F32, name="zT")
+            zT = psum_one.tile([P, L_BLOCKS, P], F32, name="zT")
             for c in range(L_BLOCKS):
                 nc.tensor.matmul_mx(
                     out=zT[:, c, :],
@@ -281,28 +281,21 @@ def tile_softmoedynamics_pb_t_e_kernel(tc, h2, logits, W3_words, W3_scales, b3, 
             nc.scalar.activation(out=y_of[t, unit][:], in_=y_of[t, unit][:], func=ACT.Exp)
 
         def add_up(t, unit):
-            if unit == 0:
-                factors = f_pool.tile([P, UNITS, GROUPS], F32, name="factors")
-                factors_of[t] = factors
+            total = small.tile([P, GROUPS], F32, name="total")
             nc.vector.tensor_reduce(
-                out=factors_of[t][:, unit, :],
-                in_=by_group(y_of[t, unit][:]),
-                axis=AXIS_X,
-                op=ALU.add,
+                out=total[:], in_=by_group(y_of[t, unit][:]), axis=AXIS_X, op=ALU.add
             )
-
-        def invert(t):
-            sums = factors_of[t][:].rearrange("p u g -> p (u g)")
-            nc.scalar.activation(out=sums, in_=sums, func=ACT.Ln)
-            nc.scalar.activation(out=sums, in_=sums, func=ACT.Exp, scale=-1.0)
+            total_of[t, unit] = total
 
         def normalise(t, unit):
-            yn = yn_pool.tile([P, L], F32, name="yn")
-            yn_of[t, unit] = yn
+            factor = small.tile([P, GROUPS], F32, name="factor")
             nc.gpsimd.tensor_tensor(
-                out=by_group(yn[:]),
+                out=factor[:], in0=total_of[t, unit][:], in1=minus_one[:], op=ALU.pow
+            )
+            nc.gpsimd.tensor_tensor(
+                out=by_group(y_of[t, unit][:]),
                 in0=by_group(y_of[t, unit][:]),
-                in1=over_group(factors_of[t][:, unit, :], GROUPS),
+                in1=over_group(factor[:], GROUPS),
                 op=ALU.mult,
             )
 
@@ -311,7 +304,7 @@ def tile_softmoedynamics_pb_t_e_kernel(tc, h2, logits, W3_words, W3_scales, b3, 
             nc.tensor.matmul(
                 out=o_ps[:],
                 lhsT=mix[:, (t // 2) * UNITS + unit, :],
-                rhs=yn_of[t, unit][:],
+                rhs=y_of[t, unit][:],
                 start=True,
                 stop=True,
             )
@@ -319,31 +312,54 @@ def tile_softmoedynamics_pb_t_e_kernel(tc, h2, logits, W3_words, W3_scales, b3, 
 
         def store_from_tensor(t, unit):
             o_sb = o_pool.tile([P, L], F32, name="o_sb")
-            nc.scalar.copy(out=o_sb[:], in_=o_ps_of[t, unit][:])
+            nc.vector.tensor_copy(out=o_sb[:], in_=o_ps_of[t, unit][:])
             first_row = (t * P + unit * ENTRIES) * AGENTS
             nc.sync.dma_start(out=out_rows[first_row : first_row + P, :], in_=o_sb[:])
 
-        def combine_on_vector(t, e):
-            if e == 0:
-                acc = acc_pool.tile([P, AGENTS, L], F32, name="acc")
-                acc_of[t] = acc
-            for n in range(AGENTS):
+        def weigh(t, n, on_scalar):
+            if (t, n) not in terms_of:
+                terms_of[t, n] = {}
+            for e in range(E):
+                if (e < SCALAR_TERMS) != on_scalar:
+                    continue
                 column = (t * AGENTS + n) * E + e
                 weight = comb[:, column : column + 1]
-                term = acc_of[t][:, n, :]
-                if e == 0:
-                    nc.scalar.activation(out=term, in_=yn_of[t, e][:], func=ACT.Copy, scale=weight)
+                term = term_pool.tile([P, L], F32, name="term")
+                terms_of[t, n][e] = term
+                if on_scalar:
+                    nc.scalar.activation(out=term[:], in_=y_of[t, e][:], func=ACT.Copy, scale=weight)
                 else:
-                    nc.vector.scalar_tensor_tensor(
-                        out=term,
-                        in0=yn_of[t, e][:],
-                        scalar=weight,
-                        in1=term,
-                        op0=ALU.mult,
-                        op1=ALU.add,
+                    nc.vector.tensor_scalar_mul(out=term[:], in0=y_of[t, e][:], scalar1=weight)
+
+        def add_terms(t, n):
+            sumT = psum.tile([P, L_BLOCKS, P], F32, name="sumT")
+            for c in range(L_BLOCKS):
+                for e in range(E):
+                    nc.tensor.matmul(
+                        out=sumT[:, c, :],
+                        lhsT=terms_of[t, n][e][:, c * P : (c + 1) * P],
+                        rhs=ident[:],
+                        is_transpose=True,
+                        start=(e == 0),
+                        stop=(e == E - 1),
                     )
-                if e == E - 1:
-                    nc.sync.dma_start(out=out[t * P : (t + 1) * P, n, :], in_=term)
+            sumT_of[t, n] = sumT
+
+        def lift(t, n):
+            sumT_sb = o_pool.tile([P, L_BLOCKS, P], F32, name="sumT_sb")
+            nc.scalar.copy(out=sumT_sb[:], in_=sumT_of[t, n][:])
+            sumT_sb_of[t, n] = sumT_sb
+
+        def turn_out(t, n):
+            o_ps = psum.tile([P, L], F32, name="o_ps")
+            for c in range(L_BLOCKS):
+                nc.tensor.transpose(o_ps[:, c * P : (c + 1) * P], sumT_sb_of[t, n][:, c, :], ident[:])
+            o_ps_of[t, n] = o_ps
+
+        def store_agent(t, n):
+            o_sb = o_pool.tile([P, L], F32, name="o_sb")
+            nc.vector.tensor_copy(out=o_sb[:], in_=o_ps_of[t, n][:])
+            nc.sync.dma_start(out=out[t * P : (t + 1) * P, n, :], in_=o_sb[:])
 
         def at(step, ahead):
             return divmod(step + ahead, UNITS)
@@ -353,51 +369,61 @@ def tile_softmoedynamics_pb_t_e_kernel(tc, h2, logits, W3_words, W3_scales, b3, 
 
         with tc.manual_schedule():
             for step in range(-LOAD, TOTAL_UNITS - STORE):
+                t, unit = at(step, ADD_BIAS)
+                if real(t):
+                    add_bias(t, unit)
                 t, unit = at(step, EXPONENT)
                 if real(t):
                     exponent(t, unit)
-                t, unit = at(step, INVERT)
-                if real(t) and unit == 0:
-                    invert(t)
-                t, unit = at(step, SHIFT)
-                if real(t):
-                    find_top(t, unit)
                 t, unit = at(step, ADD_UP)
                 if real(t):
                     add_up(t, unit)
                 t, unit = at(step, SHIFT)
                 if real(t):
-                    shift(t, unit)
+                    find_top(t, unit)
                 t, unit = at(step, NORMALISE)
                 if real(t):
                     normalise(t, unit)
+                t, unit = at(step, STORE)
+                if real(t) and not combines_on_tensor(t):
+                    store_agent(t, unit)
+                t, unit = at(step, LIFT)
+                if real(t) and combines_on_tensor(t):
+                    store_from_tensor(t, unit)
+                t, unit = at(step, SHIFT)
+                if real(t):
+                    shift(t, unit)
+                t, unit = at(step, LIFT)
+                if real(t) and not combines_on_tensor(t):
+                    lift(t, unit)
+                t, unit = at(step, WEIGH)
+                if real(t) and not combines_on_tensor(t):
+                    weigh(t, unit, True)
+                    weigh(t, unit, False)
                 t, unit = at(step, QUANTISE)
-                if real(t) and unit == 0:
-                    quantise(t)
+                if real(t) and unit % 2 == 0:
+                    quantise(t, unit // 2)
+                t, unit = at(step, REGROUP)
+                if real(t) and unit % 2 == 0:
+                    regroup(t, unit // 2)
                 t, unit = at(step, COMBINE)
                 if real(t):
                     if combines_on_tensor(t):
                         combine_on_tensor(t, unit)
                     else:
-                        combine_on_vector(t, unit)
-                t, unit = at(step, STORE)
-                if real(t) and combines_on_tensor(t):
-                    store_from_tensor(t, unit)
+                        add_terms(t, unit)
+                t, unit = at(step, TURN_OUT)
+                if real(t) and not combines_on_tensor(t):
+                    turn_out(t, unit)
                 t, unit = at(step, TURN_BACK)
                 if real(t):
                     turn_back(t, unit)
-                t, unit = at(step, ADD_BIAS)
-                if real(t):
-                    add_bias(t, unit)
                 t, unit = at(step, MULTIPLY)
                 if real(t):
                     multiply(t, unit)
-                t, unit = at(step, REGROUP)
-                if real(t) and unit < PAIRS:
-                    regroup(t, unit)
                 t, unit = at(step, TURN_H2)
-                if real(t) and unit < PAIRS:
-                    turn_h2(t, unit)
+                if real(t) and unit % 2 == 0:
+                    turn_h2(t, unit // 2)
                 t, unit = at(step, LOAD)
                 if real(t) and unit == 0:
                     load(t)

@@ -25,7 +25,7 @@ L_BLOCKS = L // P
 UNITS = 8
 ENTRIES = P // E
 TENSOR_TILES = 3
-SCALAR_TERMS = 3
+SCALAR_TERMS = 2
 
 FLOPS = 2 * B * E * K * L + 2 * B * AGENTS * E * L
 
@@ -37,21 +37,27 @@ TURN_OUT = -2
 LIFT = -1
 COMBINE = 0
 WEIGH = COMBINE + 1
-NORMALISE = WEIGH + UNITS + 1
-ADD_UP = NORMALISE
+NORMALISE = WEIGH + UNITS
+ADD_UP = NORMALISE + 1
 EXPONENT = ADD_UP + 1
-SHIFT = EXPONENT + 1
+SHIFT = EXPONENT
 TURN_BACK = SHIFT + 1
-ADD_BIAS = TURN_BACK + UNITS
+ADD_BIAS = TURN_BACK + 1
 MULTIPLY = ADD_BIAS + 1
 QUANTISE = MULTIPLY + 1
 REGROUP = QUANTISE + 1
 TURN_H2 = REGROUP + 1
-LOAD = TURN_H2 + UNITS
+LOAD = TURN_H2 + 4
+FRONT_GAIN = UNITS - 1
+GAIN_EVERY = 5
 
 
 def combines_on_tensor(t):
-    return t % 2 == 1 and t // 2 < TENSOR_TILES
+    return t >= TILES - TENSOR_TILES
+
+
+def mix_index(t, unit):
+    return (t - (TILES - TENSOR_TILES)) * UNITS + unit
 
 
 def by_group(ap):
@@ -80,108 +86,140 @@ def tile_softmoedynamics_pb_t_e_kernel(tc, h2, logits, W3_words, W3_scales, b3, 
 
         ident = const.tile([P, P], F32, name="ident")
         make_identity(nc, ident[:])
-        minus_one = const.tile([P, GROUPS], F32, name="minus_one")
-        nc.vector.memset(minus_one[:], -1.0)
 
         w_words = const.tile([P, E, 2 * L], U8, align_bytes=64, name="w_words")
-        nc.sync.dma_start(
-            out=w_words[:].bitcast(I32), in_=W3_words.bitcast(I32).rearrange("e p n -> p e n")
-        )
         w_scales = const.tile([P, E, L], U8, align_bytes=64, name="w_scales")
         nc.vector.memset(w_scales[:].rearrange("p e n -> p (e n)").bitcast(I32), 0)
-        for quadrant in range(4):
-            nc.sync.dma_start(
-                out=w_scales[32 * quadrant : 32 * quadrant + 4].bitcast(I32),
-                in_=W3_scales.bitcast(I32)[:, 4 * quadrant : 4 * quadrant + 4, :].rearrange(
-                    "e r n -> r e n"
-                ),
-            )
-
         bias_rows = const.tile([P, P], BF16, name="bias_rows")
         nc.vector.memset(bias_rows[:], 0.0)
-        nc.sync.dma_start(
-            out=bias_rows[0 : E * L_BLOCKS, :], in_=b3.rearrange("e (c l) -> (e c) l", l=P)
-        )
         bias_rows_f32 = const.tile([P, P], F32, name="bias_rows_f32")
-        nc.vector.tensor_copy(out=bias_rows_f32[:], in_=bias_rows[:])
-        bias_ps = psum.tile([P, P], F32, name="bias_ps", tag="o_ps")
-        nc.tensor.transpose(bias_ps[:], bias_rows_f32[:], ident[:])
         bias_cols = const.tile([P, P], F32, name="bias_cols")
-        nc.scalar.copy(out=bias_cols[:], in_=bias_ps[:])
 
         rows_by_entry = TILES * AGENTS
         mixes = TENSOR_TILES * UNITS
         rows = rows_by_entry + mixes
         raw = const.tile([P, rows * E], BF16, name="raw")
-        nc.sync.dma_start(
-            out=raw[:, 0 : rows_by_entry * E].rearrange("b (t c) -> b t c", t=TILES),
-            in_=logits.rearrange("(t b) n e -> b t (n e)", b=P),
-        )
-        for t in range(TILES):
-            if combines_on_tensor(t):
-                first = (rows_by_entry + (t // 2) * UNITS) * E
-                nc.sync.dma_start(
-                    out=raw[:, first : first + UNITS * E].rearrange("r (g e) -> r g e", e=E),
-                    in_=logits[t * P : (t + 1) * P].rearrange(
-                        "(g b) n e -> (b n) g e", b=ENTRIES
-                    ),
-                )
         comb = const.tile([P, rows * E], F32, name="comb")
         comb_top = const.tile([P, rows], F32, name="comb_top")
         comb_sum = const.tile([P, rows], F32, name="comb_sum")
-        nc.vector.tensor_reduce(out=comb_top[:], in_=by_group(raw[:]), axis=AXIS_X, op=ALU.max)
-        nc.vector.tensor_tensor(
-            out=by_group(comb[:]),
-            in0=by_group(raw[:]),
-            in1=over_group(comb_top[:], rows),
-            op=ALU.subtract,
-        )
-        nc.scalar.activation(out=comb[:], in_=comb[:], func=ACT.Exp)
-        nc.vector.tensor_reduce(out=comb_sum[:], in_=by_group(comb[:]), axis=AXIS_X, op=ALU.add)
-        nc.vector.reciprocal(out=comb_sum[:], in_=comb_sum[:])
-        nc.vector.tensor_tensor(
-            out=by_group(comb[:]),
-            in0=by_group(comb[:]),
-            in1=over_group(comb_sum[:], rows),
-            op=ALU.mult,
-        )
         comb_by_agent = comb[:, rows_by_entry * E :]
-
         own_entry = const.tile([P, ENTRIES], F32, name="own_entry")
-        nc.vector.tensor_reduce(
-            out=own_entry[:],
-            in_=ident[:].rearrange("p (b n) -> p b n", n=AGENTS),
-            axis=AXIS_X,
-            op=ALU.add,
-        )
         spread = const.tile([P, mixes * E, ENTRIES], F32, name="spread")
-        spread_shape = [P, mixes * E, ENTRIES]
-        nc.vector.tensor_tensor(
-            out=spread[:],
-            in0=comb_by_agent.unsqueeze(2).to_broadcast(spread_shape),
-            in1=own_entry[:].unsqueeze(1).to_broadcast(spread_shape),
-            op=ALU.mult,
-        )
         mix = const.tile([P, mixes, P], F32, name="mix")
-        for first in range(0, mixes, 4):
+        mix_ps_of = {}
+
+        def load_small_constants():
+            nc.sync.dma_start(
+                out=raw[:, 0 : rows_by_entry * E].rearrange("b (t c) -> b t c", t=TILES),
+                in_=logits.rearrange("(t b) n e -> b t (n e)", b=P),
+            )
+            nc.sync.dma_start(
+                out=bias_rows[0 : E * L_BLOCKS, :], in_=b3.rearrange("e (c l) -> (e c) l", l=P)
+            )
+            for quadrant in range(4):
+                nc.sync.dma_start(
+                    out=w_scales[32 * quadrant : 32 * quadrant + 4].bitcast(I32),
+                    in_=W3_scales.bitcast(I32)[:, 4 * quadrant : 4 * quadrant + 4, :].rearrange(
+                        "e r n -> r e n"
+                    ),
+                )
+
+        def load_words(pair):
+            nc.sync.dma_start(
+                out=w_words[:, 2 * pair : 2 * pair + 2, :].bitcast(I32),
+                in_=W3_words.bitcast(I32)[2 * pair : 2 * pair + 2].rearrange("e p n -> p e n"),
+            )
+
+        def load_logits_by_agent():
+            for t in range(TILES):
+                if combines_on_tensor(t):
+                    first = (rows_by_entry + mix_index(t, 0)) * E
+                    nc.sync.dma_start(
+                        out=raw[:, first : first + UNITS * E].rearrange("r (g e) -> r g e", e=E),
+                        in_=logits[t * P : (t + 1) * P].rearrange(
+                            "(g b) n e -> (b n) g e", b=ENTRIES
+                        ),
+                    )
+
+        def turn_bias():
+            nc.vector.tensor_copy(out=bias_rows_f32[:], in_=bias_rows[:])
+            bias_ps = psum.tile([P, P], F32, name="bias_ps", tag="o_ps")
+            nc.tensor.transpose(bias_ps[:], bias_rows_f32[:], ident[:])
+            nc.scalar.copy(out=bias_cols[:], in_=bias_ps[:])
+
+        def softmax_pieces(lo, hi):
+            columns = slice(lo * E, hi * E)
+            return [
+                lambda: nc.vector.tensor_reduce(
+                    out=comb_top[:, lo:hi], in_=by_group(raw[:, columns]), axis=AXIS_X, op=ALU.max
+                ),
+                lambda: nc.gpsimd.tensor_tensor(
+                    out=by_group(comb[:, columns]),
+                    in0=by_group(raw[:, columns]),
+                    in1=over_group(comb_top[:, lo:hi], hi - lo),
+                    op=ALU.subtract,
+                ),
+                lambda: nc.scalar.activation(out=comb[:, columns], in_=comb[:, columns], func=ACT.Exp),
+                lambda: nc.vector.tensor_reduce(
+                    out=comb_sum[:, lo:hi], in_=by_group(comb[:, columns]), axis=AXIS_X, op=ALU.add
+                ),
+                lambda: nc.vector.reciprocal(out=comb_sum[:, lo:hi], in_=comb_sum[:, lo:hi]),
+                lambda: nc.gpsimd.tensor_tensor(
+                    out=by_group(comb[:, columns]),
+                    in0=by_group(comb[:, columns]),
+                    in1=over_group(comb_sum[:, lo:hi], hi - lo),
+                    op=ALU.mult,
+                ),
+            ]
+
+        def mark_own_entry():
+            nc.vector.tensor_reduce(
+                out=own_entry[:],
+                in_=ident[:].rearrange("p (b n) -> p b n", n=AGENTS),
+                axis=AXIS_X,
+                op=ALU.add,
+            )
+
+        def spread_out(first):
+            shape = [P, 4 * E, ENTRIES]
+            nc.gpsimd.tensor_tensor(
+                out=spread[:, first * E : (first + 4) * E, :],
+                in0=comb_by_agent[:, first * E : (first + 4) * E].unsqueeze(2).to_broadcast(shape),
+                in1=own_entry[:].unsqueeze(1).to_broadcast(shape),
+                op=ALU.mult,
+            )
+
+        def turn_mix(first):
             mix_ps = psum.tile([P, 4, P], F32, name="mix_ps", tag="o_ps")
             for i in range(4):
                 unit_rows = spread[:, (first + i) * E : (first + i + 1) * E, :]
                 nc.tensor.transpose(
                     mix_ps[:, i, :], unit_rows.rearrange("p e b -> p (e b)"), ident[:]
                 )
-            nc.scalar.copy(out=mix[:, first : first + 4, :], in_=mix_ps[:])
+            mix_ps_of[first] = mix_ps
+
+        def keep_mix(first):
+            nc.scalar.copy(out=mix[:, first : first + 4, :], in_=mix_ps_of[first][:])
+
+        early_pieces = softmax_pieces(0, rows_by_entry)
+        late_pieces = [load_logits_by_agent, mark_own_entry] + softmax_pieces(rows_by_entry, rows)
+        for first in range(0, mixes, 4):
+            late_pieces.append(lambda first=first: spread_out(first))
+            late_pieces.append(lambda first=first: turn_mix(first))
+            late_pieces.append(lambda first=first: keep_mix(first))
 
         x_of, grouped_of, codes_of, h_scales_of, zT_sb_of = {}, {}, {}, {}, {}
         xt_of, zT_of, z_ps_of, top_of, y_of, total_of, o_ps_of = {}, {}, {}, {}, {}, {}, {}
-        terms_of, sumT_of, sumT_sb_of = {}, {}, {}
+        terms_of, sumT_of, sumT_sb_of, factor_of = {}, {}, {}, {}
 
-        def load(t):
-            x_sb = x_pool.tile([P, E * K], BF16, name="x_sb")
+        def load(t, pair):
+            if pair == 0:
+                x_sb = x_pool.tile([P, E * K], BF16, name="x_sb")
+                x_of[t] = x_sb
             nc.sync.dma_start(
-                out=x_sb[:], in_=h2[t * P : (t + 1) * P].rearrange("b e k -> b (e k)")
+                out=x_of[t][:, 2 * pair * K : 2 * (pair + 1) * K],
+                in_=h2[t * P : (t + 1) * P, 2 * pair : 2 * pair + 2, :].rearrange("b e k -> b (e k)"),
             )
-            x_of[t] = x_sb
 
         def turn_h2(t, pair):
             x_words = x_of[t][:].bitcast(F32)
@@ -287,15 +325,16 @@ def tile_softmoedynamics_pb_t_e_kernel(tc, h2, logits, W3_words, W3_scales, b3, 
             )
             total_of[t, unit] = total
 
-        def normalise(t, unit):
+        def invert(t, unit):
             factor = small.tile([P, GROUPS], F32, name="factor")
-            nc.gpsimd.tensor_tensor(
-                out=factor[:], in0=total_of[t, unit][:], in1=minus_one[:], op=ALU.pow
-            )
+            nc.vector.reciprocal(out=factor[:], in_=total_of[t, unit][:])
+            factor_of[t, unit] = factor
+
+        def normalise(t, unit):
             nc.gpsimd.tensor_tensor(
                 out=by_group(y_of[t, unit][:]),
                 in0=by_group(y_of[t, unit][:]),
-                in1=over_group(factor[:], GROUPS),
+                in1=over_group(factor_of[t, unit][:], GROUPS),
                 op=ALU.mult,
             )
 
@@ -303,7 +342,7 @@ def tile_softmoedynamics_pb_t_e_kernel(tc, h2, logits, W3_words, W3_scales, b3, 
             o_ps = psum.tile([P, L], F32, name="o_ps")
             nc.tensor.matmul(
                 out=o_ps[:],
-                lhsT=mix[:, (t // 2) * UNITS + unit, :],
+                lhsT=mix[:, mix_index(t, unit), :],
                 rhs=y_of[t, unit][:],
                 start=True,
                 stop=True,
@@ -312,7 +351,7 @@ def tile_softmoedynamics_pb_t_e_kernel(tc, h2, logits, W3_words, W3_scales, b3, 
 
         def store_from_tensor(t, unit):
             o_sb = o_pool.tile([P, L], F32, name="o_sb")
-            nc.vector.tensor_copy(out=o_sb[:], in_=o_ps_of[t, unit][:])
+            nc.scalar.copy(out=o_sb[:], in_=o_ps_of[t, unit][:])
             first_row = (t * P + unit * ENTRIES) * AGENTS
             nc.sync.dma_start(out=out_rows[first_row : first_row + P, :], in_=o_sb[:])
 
@@ -358,7 +397,7 @@ def tile_softmoedynamics_pb_t_e_kernel(tc, h2, logits, W3_words, W3_scales, b3, 
 
         def store_agent(t, n):
             o_sb = o_pool.tile([P, L], F32, name="o_sb")
-            nc.vector.tensor_copy(out=o_sb[:], in_=o_ps_of[t, n][:])
+            nc.scalar.copy(out=o_sb[:], in_=o_ps_of[t, n][:])
             nc.sync.dma_start(out=out[t * P : (t + 1) * P, n, :], in_=o_sb[:])
 
         def at(step, ahead):
@@ -367,45 +406,55 @@ def tile_softmoedynamics_pb_t_e_kernel(tc, h2, logits, W3_words, W3_scales, b3, 
         def real(t):
             return 0 <= t < TILES
 
+        def gained(v):
+            return min(FRONT_GAIN, max(0, (v - UNITS) // GAIN_EVERY + 1))
+
+        def front(step, ahead):
+            return [divmod(v, UNITS) for v in range(TOTAL_UNITS) if v - gained(v) - ahead == step]
+
         with tc.manual_schedule():
             for step in range(-LOAD, TOTAL_UNITS - STORE):
-                t, unit = at(step, ADD_BIAS)
-                if real(t):
+                for t, unit in front(step, ADD_BIAS):
                     add_bias(t, unit)
-                t, unit = at(step, EXPONENT)
+                t, unit = at(step, NORMALISE)
                 if real(t):
-                    exponent(t, unit)
+                    invert(t, unit)
+                    normalise(t, unit)
+                t, unit = at(step, SHIFT)
+                if real(t):
+                    find_top(t, unit)
                 t, unit = at(step, ADD_UP)
                 if real(t):
                     add_up(t, unit)
                 t, unit = at(step, SHIFT)
                 if real(t):
-                    find_top(t, unit)
-                t, unit = at(step, NORMALISE)
-                if real(t):
-                    normalise(t, unit)
+                    shift(t, unit)
                 t, unit = at(step, STORE)
                 if real(t) and not combines_on_tensor(t):
                     store_agent(t, unit)
                 t, unit = at(step, LIFT)
-                if real(t) and combines_on_tensor(t):
-                    store_from_tensor(t, unit)
-                t, unit = at(step, SHIFT)
                 if real(t):
-                    shift(t, unit)
-                t, unit = at(step, LIFT)
-                if real(t) and not combines_on_tensor(t):
-                    lift(t, unit)
+                    if combines_on_tensor(t):
+                        store_from_tensor(t, unit)
+                    else:
+                        lift(t, unit)
                 t, unit = at(step, WEIGH)
                 if real(t) and not combines_on_tensor(t):
                     weigh(t, unit, True)
                     weigh(t, unit, False)
-                t, unit = at(step, QUANTISE)
-                if real(t) and unit % 2 == 0:
-                    quantise(t, unit // 2)
-                t, unit = at(step, REGROUP)
-                if real(t) and unit % 2 == 0:
-                    regroup(t, unit // 2)
+                for t, unit in front(step, QUANTISE):
+                    if unit % 2 == 0:
+                        quantise(t, unit // 2)
+                if 0 <= step + LOAD - 1 < len(early_pieces):
+                    early_pieces[step + LOAD - 1]()
+                if 0 <= step < len(late_pieces):
+                    late_pieces[step]()
+                for t, unit in front(step, REGROUP):
+                    if unit % 2 == 0:
+                        regroup(t, unit // 2)
+                t, unit = at(step, EXPONENT)
+                if real(t):
+                    exponent(t, unit)
                 t, unit = at(step, COMBINE)
                 if real(t):
                     if combines_on_tensor(t):
@@ -418,12 +467,17 @@ def tile_softmoedynamics_pb_t_e_kernel(tc, h2, logits, W3_words, W3_scales, b3, 
                 t, unit = at(step, TURN_BACK)
                 if real(t):
                     turn_back(t, unit)
-                t, unit = at(step, MULTIPLY)
-                if real(t):
+                for t, unit in front(step, MULTIPLY):
                     multiply(t, unit)
-                t, unit = at(step, TURN_H2)
-                if real(t) and unit % 2 == 0:
-                    turn_h2(t, unit // 2)
-                t, unit = at(step, LOAD)
-                if real(t) and unit == 0:
-                    load(t)
+                for t, unit in front(step, TURN_H2):
+                    if unit % 2 == 0:
+                        turn_h2(t, unit // 2)
+                if step == -TURN_H2:
+                    turn_bias()
+                for t, unit in front(step, LOAD):
+                    if unit % 2 == 0:
+                        load(t, unit // 2)
+                        if t == 0:
+                            if unit == 0:
+                                load_small_constants()
+                            load_words(unit // 2)

@@ -48,6 +48,7 @@ QUANTISE = MULTIPLY + 1
 REGROUP = QUANTISE + 1
 TURN_H2 = REGROUP + 1
 LOAD = TURN_H2 + 4
+SET_UP = 1 - LOAD
 FRONT_GAIN = UNITS - 1
 GAIN_EVERY = 5
 
@@ -143,7 +144,7 @@ def tile_softmoedynamics_pb_t_e_kernel(tc, h2, logits, W3_words, W3_scales, b3, 
 
         def turn_bias():
             nc.vector.tensor_copy(out=bias_rows_f32[:], in_=bias_rows[:])
-            bias_ps = psum.tile([P, P], F32, name="bias_ps", tag="o_ps")
+            bias_ps = psum_one.tile([P, P], F32, name="bias_ps", tag="o_ps")
             nc.tensor.transpose(bias_ps[:], bias_rows_f32[:], ident[:])
             nc.scalar.copy(out=bias_cols[:], in_=bias_ps[:])
 
@@ -190,7 +191,7 @@ def tile_softmoedynamics_pb_t_e_kernel(tc, h2, logits, W3_words, W3_scales, b3, 
             )
 
         def turn_mix(first):
-            mix_ps = psum.tile([P, 4, P], F32, name="mix_ps", tag="o_ps")
+            mix_ps = psum_one.tile([P, 4, P], F32, name="mix_ps", tag="o_ps")
             for i in range(4):
                 unit_rows = spread[:, (first + i) * E : (first + i + 1) * E, :]
                 nc.tensor.transpose(
@@ -201,12 +202,20 @@ def tile_softmoedynamics_pb_t_e_kernel(tc, h2, logits, W3_words, W3_scales, b3, 
         def keep_mix(first):
             nc.scalar.copy(out=mix[:, first : first + 4, :], in_=mix_ps_of[first][:])
 
-        early_pieces = softmax_pieces(0, rows_by_entry)
-        late_pieces = [load_logits_by_agent, mark_own_entry] + softmax_pieces(rows_by_entry, rows)
-        for first in range(0, mixes, 4):
-            late_pieces.append(lambda first=first: spread_out(first))
-            late_pieces.append(lambda first=first: turn_mix(first))
-            late_pieces.append(lambda first=first: keep_mix(first))
+        plan = {}
+
+        def plan_at(step, piece):
+            plan.setdefault(step, []).append(piece)
+
+        for i, piece in enumerate(softmax_pieces(0, rows_by_entry)):
+            plan_at(SET_UP + i, piece)
+        plan_at(SET_UP + 2, mark_own_entry)
+        for i, piece in enumerate(softmax_pieces(rows_by_entry, rows)):
+            plan_at(SET_UP + 3 + i, piece)
+        for i in range(mixes // 4):
+            plan_at(SET_UP + 9 + 2 * i, lambda i=i: spread_out(4 * i))
+            plan_at(SET_UP + 10 + 2 * i, lambda i=i: turn_mix(4 * i))
+            plan_at(SET_UP + 11 + 2 * i, lambda i=i: keep_mix(4 * i))
 
         x_of, grouped_of, codes_of, h_scales_of, zT_sb_of = {}, {}, {}, {}, {}
         xt_of, zT_of, z_ps_of, top_of, y_of, total_of, o_ps_of = {}, {}, {}, {}, {}, {}, {}
@@ -257,7 +266,7 @@ def tile_softmoedynamics_pb_t_e_kernel(tc, h2, logits, W3_words, W3_scales, b3, 
 
         def multiply(t, e):
             batch = slice(e * P, (e + 1) * P)
-            zT = psum_one.tile([P, L_BLOCKS, P], F32, name="zT")
+            zT = psum.tile([P, L_BLOCKS, P], F32, name="zT")
             for c in range(L_BLOCKS):
                 nc.tensor.matmul_mx(
                     out=zT[:, c, :],
@@ -339,7 +348,7 @@ def tile_softmoedynamics_pb_t_e_kernel(tc, h2, logits, W3_words, W3_scales, b3, 
             )
 
         def combine_on_tensor(t, unit):
-            o_ps = psum.tile([P, L], F32, name="o_ps")
+            o_ps = psum.tile([P, L], F32, name="o_ps", tag="sumT")
             nc.tensor.matmul(
                 out=o_ps[:],
                 lhsT=mix[:, mix_index(t, unit), :],
@@ -390,7 +399,7 @@ def tile_softmoedynamics_pb_t_e_kernel(tc, h2, logits, W3_words, W3_scales, b3, 
             sumT_sb_of[t, n] = sumT_sb
 
         def turn_out(t, n):
-            o_ps = psum.tile([P, L], F32, name="o_ps")
+            o_ps = psum_one.tile([P, L], F32, name="o_ps")
             for c in range(L_BLOCKS):
                 nc.tensor.transpose(o_ps[:, c * P : (c + 1) * P], sumT_sb_of[t, n][:, c, :], ident[:])
             o_ps_of[t, n] = o_ps
@@ -445,10 +454,8 @@ def tile_softmoedynamics_pb_t_e_kernel(tc, h2, logits, W3_words, W3_scales, b3, 
                 for t, unit in front(step, QUANTISE):
                     if unit % 2 == 0:
                         quantise(t, unit // 2)
-                if 0 <= step + LOAD - 1 < len(early_pieces):
-                    early_pieces[step + LOAD - 1]()
-                if 0 <= step < len(late_pieces):
-                    late_pieces[step]()
+                for piece in plan.get(step, []):
+                    piece()
                 for t, unit in front(step, REGROUP):
                     if unit % 2 == 0:
                         regroup(t, unit // 2)
@@ -456,11 +463,8 @@ def tile_softmoedynamics_pb_t_e_kernel(tc, h2, logits, W3_words, W3_scales, b3, 
                 if real(t):
                     exponent(t, unit)
                 t, unit = at(step, COMBINE)
-                if real(t):
-                    if combines_on_tensor(t):
-                        combine_on_tensor(t, unit)
-                    else:
-                        add_terms(t, unit)
+                if real(t) and not combines_on_tensor(t):
+                    add_terms(t, unit)
                 t, unit = at(step, TURN_OUT)
                 if real(t) and not combines_on_tensor(t):
                     turn_out(t, unit)
@@ -468,12 +472,17 @@ def tile_softmoedynamics_pb_t_e_kernel(tc, h2, logits, W3_words, W3_scales, b3, 
                 if real(t):
                     turn_back(t, unit)
                 for t, unit in front(step, MULTIPLY):
-                    multiply(t, unit)
+                    if unit % 2 == 0:
+                        multiply(t, unit)
+                        multiply(t, unit + 1)
                 for t, unit in front(step, TURN_H2):
                     if unit % 2 == 0:
                         turn_h2(t, unit // 2)
                 if step == -TURN_H2:
                     turn_bias()
+                t, unit = at(step, COMBINE)
+                if real(t) and combines_on_tensor(t):
+                    combine_on_tensor(t, unit)
                 for t, unit in front(step, LOAD):
                     if unit % 2 == 0:
                         load(t, unit // 2)
@@ -481,3 +490,5 @@ def tile_softmoedynamics_pb_t_e_kernel(tc, h2, logits, W3_words, W3_scales, b3, 
                             if unit == 0:
                                 load_small_constants()
                             load_words(unit // 2)
+                            if unit == 2:
+                                load_logits_by_agent()

@@ -49,6 +49,7 @@ REGROUP = QUANTISE + 1
 TURN_H2 = REGROUP + 1
 LOAD = TURN_H2 + 4
 SET_UP = 1 - LOAD
+CATCH_UP = (5, 8)
 FRONT_GAIN = UNITS - 1
 GAIN_EVERY = 5
 
@@ -59,6 +60,14 @@ def combines_on_tensor(t):
 
 def mix_index(t, unit):
     return (t - (TILES - TENSOR_TILES)) * UNITS + unit
+
+
+def scalar_terms(n):
+    return SCALAR_TERMS + n % 2
+
+
+def folded(n):
+    return n % 2
 
 
 def by_group(ap):
@@ -79,7 +88,7 @@ def tile_softmoedynamics_pb_t_e_kernel(tc, h2, logits, W3_words, W3_scales, b3, 
         quant = ctx.enter_context(tc.tile_pool(name="quant", bufs=2))
         z_pool = ctx.enter_context(tc.tile_pool(name="z", bufs=2))
         y_pool = ctx.enter_context(tc.tile_pool(name="y", bufs=SHIFT + UNITS))
-        term_pool = ctx.enter_context(tc.tile_pool(name="term", bufs=2 * E))
+        term_pool = ctx.enter_context(tc.tile_pool(name="term", bufs=2 * E - 1))
         o_pool = ctx.enter_context(tc.tile_pool(name="o", bufs=3))
         small = ctx.enter_context(tc.tile_pool(name="small", bufs=3))
         psum_one = ctx.enter_context(tc.psum_pool(name="psum_one", bufs=1))
@@ -368,10 +377,16 @@ def tile_softmoedynamics_pb_t_e_kernel(tc, h2, logits, W3_words, W3_scales, b3, 
             if (t, n) not in terms_of:
                 terms_of[t, n] = {}
             for e in range(E):
-                if (e < SCALAR_TERMS) != on_scalar:
+                if (e < scalar_terms(n)) != on_scalar:
                     continue
                 column = (t * AGENTS + n) * E + e
                 weight = comb[:, column : column + 1]
+                if e >= E - folded(n):
+                    term = terms_of[t, n][scalar_terms(n)]
+                    nc.vector.scalar_tensor_tensor(
+                        out=term[:], in0=y_of[t, e][:], scalar=weight, in1=term[:], op0=ALU.mult, op1=ALU.add
+                    )
+                    continue
                 term = term_pool.tile([P, L], F32, name="term")
                 terms_of[t, n][e] = term
                 if on_scalar:
@@ -382,14 +397,14 @@ def tile_softmoedynamics_pb_t_e_kernel(tc, h2, logits, W3_words, W3_scales, b3, 
         def add_terms(t, n):
             sumT = psum.tile([P, L_BLOCKS, P], F32, name="sumT")
             for c in range(L_BLOCKS):
-                for e in range(E):
+                for e in range(E - folded(n)):
                     nc.tensor.matmul(
                         out=sumT[:, c, :],
                         lhsT=terms_of[t, n][e][:, c * P : (c + 1) * P],
                         rhs=ident[:],
                         is_transpose=True,
                         start=(e == 0),
-                        stop=(e == E - 1),
+                        stop=(e == E - folded(n) - 1),
                     )
             sumT_of[t, n] = sumT
 
@@ -421,6 +436,15 @@ def tile_softmoedynamics_pb_t_e_kernel(tc, h2, logits, W3_words, W3_scales, b3, 
         def front(step, ahead):
             return [divmod(v, UNITS) for v in range(TOTAL_UNITS) if v - gained(v) - ahead == step]
 
+        first_mixed = (TILES - TENSOR_TILES) * UNITS
+
+        def mixed_at(v):
+            steps, units = CATCH_UP
+            return max(v - NORMALISE + 1, first_mixed + ((v - first_mixed) * steps + units - 1) // units)
+
+        def mixed(step):
+            return [divmod(v, UNITS) for v in range(first_mixed, TOTAL_UNITS) if mixed_at(v) == step]
+
         with tc.manual_schedule():
             for step in range(-LOAD, TOTAL_UNITS - STORE):
                 for t, unit in front(step, ADD_BIAS):
@@ -441,12 +465,11 @@ def tile_softmoedynamics_pb_t_e_kernel(tc, h2, logits, W3_words, W3_scales, b3, 
                 t, unit = at(step, STORE)
                 if real(t) and not combines_on_tensor(t):
                     store_agent(t, unit)
+                for t, unit in mixed(step + LIFT):
+                    store_from_tensor(t, unit)
                 t, unit = at(step, LIFT)
-                if real(t):
-                    if combines_on_tensor(t):
-                        store_from_tensor(t, unit)
-                    else:
-                        lift(t, unit)
+                if real(t) and not combines_on_tensor(t):
+                    lift(t, unit)
                 t, unit = at(step, WEIGH)
                 if real(t) and not combines_on_tensor(t):
                     weigh(t, unit, True)
@@ -480,8 +503,7 @@ def tile_softmoedynamics_pb_t_e_kernel(tc, h2, logits, W3_words, W3_scales, b3, 
                         turn_h2(t, unit // 2)
                 if step == -TURN_H2:
                     turn_bias()
-                t, unit = at(step, COMBINE)
-                if real(t) and combines_on_tensor(t):
+                for t, unit in mixed(step):
                     combine_on_tensor(t, unit)
                 for t, unit in front(step, LOAD):
                     if unit % 2 == 0:

@@ -485,15 +485,15 @@ def tile_softmoedynamics_pb_t_e_kernel(tc, h2, logits, W3_words, W3_scales, b3, 
                 t, unit = at(step, EXPONENT)
                 if real(t):
                     exponent(t, unit)
+                t, unit = at(step, TURN_BACK)
+                if real(t):
+                    turn_back(t, unit)
                 t, unit = at(step, COMBINE)
                 if real(t) and not combines_on_tensor(t):
                     add_terms(t, unit)
                 t, unit = at(step, TURN_OUT)
                 if real(t) and not combines_on_tensor(t):
                     turn_out(t, unit)
-                t, unit = at(step, TURN_BACK)
-                if real(t):
-                    turn_back(t, unit)
                 for t, unit in front(step, MULTIPLY):
                     if unit % 2 == 0:
                         multiply(t, unit)

@@ -25,7 +25,8 @@ L_BLOCKS = L // P
 UNITS = 8
 ENTRIES = P // E
 TENSOR_TILES = 3
-SCALAR_TERMS = 2
+ADDED = E - 1
+SCALAR_TERMS = 3
 
 FLOPS = 2 * B * E * K * L + 2 * B * AGENTS * E * L
 
@@ -48,7 +49,9 @@ QUANTISE = MULTIPLY + 1
 REGROUP = QUANTISE + 1
 TURN_H2 = REGROUP + 1
 LOAD = TURN_H2 + 4
-SET_UP = 1 - LOAD
+AGENT_SOFTMAX = (-MULTIPLY, -MULTIPLY, -ADD_BIAS, -TURN_BACK, -TURN_BACK, -TURN_BACK)
+ENTRY_SOFTMAX = (-ADD_BIAS, -ADD_BIAS, -TURN_BACK, -SHIFT, -SHIFT, -SHIFT)
+SPREAD = -TURN_BACK
 CATCH_UP = (5, 8)
 FRONT_GAIN = UNITS - 1
 GAIN_EVERY = 5
@@ -63,11 +66,7 @@ def mix_index(t, unit):
 
 
 def scalar_terms(n):
-    return SCALAR_TERMS + n % 2
-
-
-def folded(n):
-    return n % 2
+    return SCALAR_TERMS + n % 4 // 3
 
 
 def by_group(ap):
@@ -86,9 +85,10 @@ def tile_softmoedynamics_pb_t_e_kernel(tc, h2, logits, W3_words, W3_scales, b3, 
         const = ctx.enter_context(tc.tile_pool(name="const", bufs=1))
         x_pool = ctx.enter_context(tc.tile_pool(name="x", bufs=2))
         quant = ctx.enter_context(tc.tile_pool(name="quant", bufs=2))
-        z_pool = ctx.enter_context(tc.tile_pool(name="z", bufs=2))
-        y_pool = ctx.enter_context(tc.tile_pool(name="y", bufs=SHIFT + UNITS))
-        term_pool = ctx.enter_context(tc.tile_pool(name="term", bufs=2 * E - 1))
+        half_pool = ctx.enter_context(tc.tile_pool(name="half", bufs=2))
+        z_pool = ctx.enter_context(tc.tile_pool(name="z", bufs=3))
+        y_pool = ctx.enter_context(tc.tile_pool(name="y", bufs=SHIFT + UNITS + 3))
+        term_pool = ctx.enter_context(tc.tile_pool(name="term", bufs=2 * ADDED))
         o_pool = ctx.enter_context(tc.tile_pool(name="o", bufs=3))
         small = ctx.enter_context(tc.tile_pool(name="small", bufs=3))
         psum_one = ctx.enter_context(tc.psum_pool(name="psum_one", bufs=1))
@@ -118,11 +118,13 @@ def tile_softmoedynamics_pb_t_e_kernel(tc, h2, logits, W3_words, W3_scales, b3, 
         mix = const.tile([P, mixes, P], F32, name="mix")
         mix_ps_of = {}
 
-        def load_small_constants():
+        def load_logits_by_entry():
             nc.sync.dma_start(
                 out=raw[:, 0 : rows_by_entry * E].rearrange("b (t c) -> b t c", t=TILES),
                 in_=logits.rearrange("(t b) n e -> b t (n e)", b=P),
             )
+
+        def load_bias_and_scales():
             nc.sync.dma_start(
                 out=bias_rows[0 : E * L_BLOCKS, :], in_=b3.rearrange("e (c l) -> (e c) l", l=P)
             )
@@ -141,21 +143,21 @@ def tile_softmoedynamics_pb_t_e_kernel(tc, h2, logits, W3_words, W3_scales, b3, 
             )
 
         def load_logits_by_agent():
-            for t in range(TILES):
-                if combines_on_tensor(t):
-                    first = (rows_by_entry + mix_index(t, 0)) * E
-                    nc.sync.dma_start(
-                        out=raw[:, first : first + UNITS * E].rearrange("r (g e) -> r g e", e=E),
-                        in_=logits[t * P : (t + 1) * P].rearrange(
-                            "(g b) n e -> (b n) g e", b=ENTRIES
-                        ),
-                    )
+            nc.sync.dma_start(
+                out=raw[:, rows_by_entry * E :].rearrange("r (g e) -> r g e", e=E),
+                in_=logits[(TILES - TENSOR_TILES) * P :].rearrange("(g b) n e -> (b n) g e", b=ENTRIES),
+            )
+
+        def widen_bias():
+            nc.vector.tensor_copy(out=bias_rows_f32[:], in_=bias_rows[:])
 
         def turn_bias():
-            nc.vector.tensor_copy(out=bias_rows_f32[:], in_=bias_rows[:])
             bias_ps = psum_one.tile([P, P], F32, name="bias_ps", tag="o_ps")
             nc.tensor.transpose(bias_ps[:], bias_rows_f32[:], ident[:])
-            nc.scalar.copy(out=bias_cols[:], in_=bias_ps[:])
+            mix_ps_of["bias"] = bias_ps
+
+        def keep_bias():
+            nc.scalar.copy(out=bias_cols[:], in_=mix_ps_of["bias"][:])
 
         def softmax_pieces(lo, hi):
             columns = slice(lo * E, hi * E)
@@ -163,7 +165,7 @@ def tile_softmoedynamics_pb_t_e_kernel(tc, h2, logits, W3_words, W3_scales, b3, 
                 lambda: nc.vector.tensor_reduce(
                     out=comb_top[:, lo:hi], in_=by_group(raw[:, columns]), axis=AXIS_X, op=ALU.max
                 ),
-                lambda: nc.gpsimd.tensor_tensor(
+                lambda: nc.vector.tensor_tensor(
                     out=by_group(comb[:, columns]),
                     in0=by_group(raw[:, columns]),
                     in1=over_group(comb_top[:, lo:hi], hi - lo),
@@ -174,7 +176,7 @@ def tile_softmoedynamics_pb_t_e_kernel(tc, h2, logits, W3_words, W3_scales, b3, 
                     out=comb_sum[:, lo:hi], in_=by_group(comb[:, columns]), axis=AXIS_X, op=ALU.add
                 ),
                 lambda: nc.vector.reciprocal(out=comb_sum[:, lo:hi], in_=comb_sum[:, lo:hi]),
-                lambda: nc.gpsimd.tensor_tensor(
+                lambda: nc.vector.tensor_tensor(
                     out=by_group(comb[:, columns]),
                     in0=by_group(comb[:, columns]),
                     in1=over_group(comb_sum[:, lo:hi], hi - lo),
@@ -211,24 +213,27 @@ def tile_softmoedynamics_pb_t_e_kernel(tc, h2, logits, W3_words, W3_scales, b3, 
         def keep_mix(first):
             nc.scalar.copy(out=mix[:, first : first + 4, :], in_=mix_ps_of[first][:])
 
-        plan = {}
+        plan, turns = {}, {}
 
         def plan_at(step, piece):
             plan.setdefault(step, []).append(piece)
 
-        for i, piece in enumerate(softmax_pieces(0, rows_by_entry)):
-            plan_at(SET_UP + i, piece)
-        plan_at(SET_UP + 2, mark_own_entry)
-        for i, piece in enumerate(softmax_pieces(rows_by_entry, rows)):
-            plan_at(SET_UP + 3 + i, piece)
+        plan_at(-TURN_H2, widen_bias)
+        turns[-REGROUP] = [turn_bias]
+        plan_at(-MULTIPLY, keep_bias)
+        for step, piece in zip(AGENT_SOFTMAX, softmax_pieces(rows_by_entry, rows)):
+            plan_at(step, piece)
+        for step, piece in zip(ENTRY_SOFTMAX, softmax_pieces(0, rows_by_entry)):
+            plan_at(step, piece)
+        plan_at(-TURN_BACK, mark_own_entry)
         for i in range(mixes // 4):
-            plan_at(SET_UP + 9 + 2 * i, lambda i=i: spread_out(4 * i))
-            plan_at(SET_UP + 10 + 2 * i, lambda i=i: turn_mix(4 * i))
-            plan_at(SET_UP + 11 + 2 * i, lambda i=i: keep_mix(4 * i))
+            plan_at(SPREAD + i, lambda i=i: spread_out(4 * i))
+            turns.setdefault(SPREAD + i + 1, []).append(lambda i=i: turn_mix(4 * i))
+            plan_at(SPREAD + i + 2, lambda i=i: keep_mix(4 * i))
 
         x_of, grouped_of, codes_of, h_scales_of, zT_sb_of = {}, {}, {}, {}, {}
         xt_of, zT_of, z_ps_of, top_of, y_of, total_of, o_ps_of = {}, {}, {}, {}, {}, {}, {}
-        terms_of, sumT_of, sumT_sb_of, factor_of = {}, {}, {}, {}
+        terms_of, sumT_of, sumT_sb_of, factor_of, half_of = {}, {}, {}, {}, {}
 
         def load(t, pair):
             if pair == 0:
@@ -336,11 +341,17 @@ def tile_softmoedynamics_pb_t_e_kernel(tc, h2, logits, W3_words, W3_scales, b3, 
         def exponent(t, unit):
             nc.scalar.activation(out=y_of[t, unit][:], in_=y_of[t, unit][:], func=ACT.Exp)
 
+        def halve(t, unit):
+            half = half_pool.tile([P, GROUPS, GROUP // 2], F32, name="half")
+            eights = by_group(y_of[t, unit][:])
+            nc.gpsimd.tensor_tensor(
+                out=half[:], in0=eights[:, :, 0 : GROUP // 2], in1=eights[:, :, GROUP // 2 : GROUP], op=ALU.add
+            )
+            half_of[t, unit] = half
+
         def add_up(t, unit):
             total = small.tile([P, GROUPS], F32, name="total")
-            nc.vector.tensor_reduce(
-                out=total[:], in_=by_group(y_of[t, unit][:]), axis=AXIS_X, op=ALU.add
-            )
+            nc.vector.tensor_reduce(out=total[:], in_=half_of[t, unit][:], axis=AXIS_X, op=ALU.add)
             total_of[t, unit] = total
 
         def invert(t, unit):
@@ -373,20 +384,17 @@ def tile_softmoedynamics_pb_t_e_kernel(tc, h2, logits, W3_words, W3_scales, b3, 
             first_row = (t * P + unit * ENTRIES) * AGENTS
             nc.sync.dma_start(out=out_rows[first_row : first_row + P, :], in_=o_sb[:])
 
+        def weight_of(t, n, e):
+            column = (t * AGENTS + n) * E + e
+            return comb[:, column : column + 1]
+
         def weigh(t, n, on_scalar):
             if (t, n) not in terms_of:
                 terms_of[t, n] = {}
-            for e in range(E):
+            for e in range(ADDED):
                 if (e < scalar_terms(n)) != on_scalar:
                     continue
-                column = (t * AGENTS + n) * E + e
-                weight = comb[:, column : column + 1]
-                if e >= E - folded(n):
-                    term = terms_of[t, n][scalar_terms(n)]
-                    nc.vector.scalar_tensor_tensor(
-                        out=term[:], in0=y_of[t, e][:], scalar=weight, in1=term[:], op0=ALU.mult, op1=ALU.add
-                    )
-                    continue
+                weight = weight_of(t, n, e)
                 term = term_pool.tile([P, L], F32, name="term")
                 terms_of[t, n][e] = term
                 if on_scalar:
@@ -397,14 +405,14 @@ def tile_softmoedynamics_pb_t_e_kernel(tc, h2, logits, W3_words, W3_scales, b3, 
         def add_terms(t, n):
             sumT = psum.tile([P, L_BLOCKS, P], F32, name="sumT")
             for c in range(L_BLOCKS):
-                for e in range(E - folded(n)):
+                for e in range(ADDED):
                     nc.tensor.matmul(
                         out=sumT[:, c, :],
                         lhsT=terms_of[t, n][e][:, c * P : (c + 1) * P],
                         rhs=ident[:],
                         is_transpose=True,
                         start=(e == 0),
-                        stop=(e == E - folded(n) - 1),
+                        stop=(e == ADDED - 1),
                     )
             sumT_of[t, n] = sumT
 
@@ -421,7 +429,14 @@ def tile_softmoedynamics_pb_t_e_kernel(tc, h2, logits, W3_words, W3_scales, b3, 
 
         def store_agent(t, n):
             o_sb = o_pool.tile([P, L], F32, name="o_sb")
-            nc.scalar.copy(out=o_sb[:], in_=o_ps_of[t, n][:])
+            nc.vector.scalar_tensor_tensor(
+                out=o_sb[:],
+                in0=y_of[t, E - 1][:],
+                scalar=weight_of(t, n, E - 1),
+                in1=o_ps_of[t, n][:],
+                op0=ALU.mult,
+                op1=ALU.add,
+            )
             nc.sync.dma_start(out=out[t * P : (t + 1) * P, n, :], in_=o_sb[:])
 
         def at(step, ahead):
@@ -431,7 +446,7 @@ def tile_softmoedynamics_pb_t_e_kernel(tc, h2, logits, W3_words, W3_scales, b3, 
             return 0 <= t < TILES
 
         def gained(v):
-            return min(FRONT_GAIN, max(0, (v - UNITS) // GAIN_EVERY + 1))
+            return min(FRONT_GAIN, max(0, (v - 4) // 2 + 1))
 
         def front(step, ahead):
             return [divmod(v, UNITS) for v in range(TOTAL_UNITS) if v - gained(v) - ahead == step]
@@ -449,6 +464,9 @@ def tile_softmoedynamics_pb_t_e_kernel(tc, h2, logits, W3_words, W3_scales, b3, 
             for step in range(-LOAD, TOTAL_UNITS - STORE):
                 for t, unit in front(step, ADD_BIAS):
                     add_bias(t, unit)
+                t, unit = at(step, ADD_UP)
+                if real(t):
+                    halve(t, unit)
                 t, unit = at(step, NORMALISE)
                 if real(t):
                     invert(t, unit)
@@ -456,15 +474,15 @@ def tile_softmoedynamics_pb_t_e_kernel(tc, h2, logits, W3_words, W3_scales, b3, 
                 t, unit = at(step, SHIFT)
                 if real(t):
                     find_top(t, unit)
-                t, unit = at(step, ADD_UP)
-                if real(t):
-                    add_up(t, unit)
-                t, unit = at(step, SHIFT)
-                if real(t):
-                    shift(t, unit)
                 t, unit = at(step, STORE)
                 if real(t) and not combines_on_tensor(t):
                     store_agent(t, unit)
+                t, unit = at(step, SHIFT)
+                if real(t):
+                    shift(t, unit)
+                t, unit = at(step, ADD_UP)
+                if real(t):
+                    add_up(t, unit)
                 for t, unit in mixed(step + LIFT):
                     store_from_tensor(t, unit)
                 t, unit = at(step, LIFT)
@@ -494,6 +512,8 @@ def tile_softmoedynamics_pb_t_e_kernel(tc, h2, logits, W3_words, W3_scales, b3, 
                 t, unit = at(step, TURN_OUT)
                 if real(t) and not combines_on_tensor(t):
                     turn_out(t, unit)
+                for piece in turns.get(step, []):
+                    piece()
                 for t, unit in front(step, MULTIPLY):
                     if unit % 2 == 0:
                         multiply(t, unit)
@@ -501,16 +521,18 @@ def tile_softmoedynamics_pb_t_e_kernel(tc, h2, logits, W3_words, W3_scales, b3, 
                 for t, unit in front(step, TURN_H2):
                     if unit % 2 == 0:
                         turn_h2(t, unit // 2)
-                if step == -TURN_H2:
-                    turn_bias()
                 for t, unit in mixed(step):
                     combine_on_tensor(t, unit)
                 for t, unit in front(step, LOAD):
                     if unit % 2 == 0:
                         load(t, unit // 2)
                         if t == 0:
-                            if unit == 0:
-                                load_small_constants()
-                            load_words(unit // 2)
                             if unit == 2:
+                                load_bias_and_scales()
+                                load_words(0)
                                 load_logits_by_agent()
+                                load_logits_by_entry()
+                            if unit >= 4:
+                                load_words(unit // 2 - 1)
+                            if unit == 6:
+                                load_words(3)

from contextlib import ExitStack

import concourse.mybir as mybir
from concourse.masks import make_identity

F32 = mybir.dt.float32
BF16 = mybir.dt.bfloat16
I32 = mybir.dt.int32
U32 = mybir.dt.uint32
U8 = mybir.dt.uint8
FP8X4 = mybir.dt.float8_e4m3fn_x4
FP4X4 = mybir.dt.float4_e2m1fn_x4
ALU = mybir.AluOpType
ACT = mybir.ActivationFunctionType
AXIS_X = mybir.AxisListType.X

P = 128
PACK = 4
B, AGENTS, E, K, L = 1024, 8, 8, 512, 512
GROUP = 8
GROUPS = L // GROUP
TILES = B // P
WORDS = K // 2
L_BLOCKS = L // P
UNITS = 8
ENTRIES = P // E
TENSOR_TILES = 3
ADDED = E - 1
SCALAR_TERMS = 3

FLOPS = 2 * B * E * K * L + 2 * B * AGENTS * E * L

TOTAL_UNITS = TILES * UNITS
PAIRS = E // 2

STORE = -3
TURN_OUT = -2
LIFT = -1
COMBINE = 0
WEIGH = COMBINE + 1
NORMALISE = WEIGH + UNITS
ADD_UP = NORMALISE + 1
EXPONENT = ADD_UP + 1
SHIFT = EXPONENT
TURN_BACK = SHIFT + 1
ADD_BIAS = TURN_BACK + 1
MULTIPLY = ADD_BIAS + 1
QUANTISE = MULTIPLY + 1
REGROUP = QUANTISE + 1
TURN_H2 = REGROUP + 1
LOAD = TURN_H2 + 4
AGENT_SOFTMAX = (-MULTIPLY, -MULTIPLY, -ADD_BIAS, -TURN_BACK, -TURN_BACK, -TURN_BACK)
ENTRY_SOFTMAX = (-ADD_BIAS, -ADD_BIAS, -TURN_BACK, -SHIFT, -SHIFT, -SHIFT)
SPREAD = -TURN_BACK
CATCH_UP = (5, 8)
FRONT_GAIN = UNITS - 1
GAIN_EVERY = 5


def combines_on_tensor(t):
    return t >= TILES - TENSOR_TILES


def mix_index(t, unit):
    return (t - (TILES - TENSOR_TILES)) * UNITS + unit


def scalar_terms(n):
    return SCALAR_TERMS + n % 4 // 3


def by_group(ap):
    return ap.rearrange("p (g j) -> p g j", j=GROUP)


def over_group(ap, groups):
    return ap.unsqueeze(2).to_broadcast([P, groups, GROUP])


def tile_softmoedynamics_pb_t_e_kernel(tc, h2, logits, W3_words, W3_scales, b3, out):
    nc = tc.nc
    out_rows = out.rearrange("b n l -> (b n) l")

    with ExitStack() as ctx:
        const = ctx.enter_context(tc.tile_pool(name="const", bufs=1))
        x_pool = ctx.enter_context(tc.tile_pool(name="x", bufs=2))
        quant = ctx.enter_context(tc.tile_pool(name="quant", bufs=2))
        half_pool = ctx.enter_context(tc.tile_pool(name="half", bufs=2))
        z_pool = ctx.enter_context(tc.tile_pool(name="z", bufs=3))
        y_pool = ctx.enter_context(tc.tile_pool(name="y", bufs=SHIFT + UNITS + 3))
        term_pool = ctx.enter_context(tc.tile_pool(name="term", bufs=2 * ADDED))
        o_pool = ctx.enter_context(tc.tile_pool(name="o", bufs=3))
        small = ctx.enter_context(tc.tile_pool(name="small", bufs=3))
        psum_one = ctx.enter_context(tc.psum_pool(name="psum_one", bufs=1))
        psum = ctx.enter_context(tc.psum_pool(name="psum", bufs=2))

        ident = const.tile([P, P], F32, name="ident")
        make_identity(nc, ident[:])

        w_words = const.tile([P, E, 2 * L], U8, align_bytes=64, name="w_words")
        w_scales = const.tile([P, E, L], U8, align_bytes=64, name="w_scales")
        nc.vector.memset(w_scales[:].rearrange("p e n -> p (e n)").bitcast(I32), 0)
        bias_rows = const.tile([P, P], BF16, name="bias_rows")
        nc.vector.memset(bias_rows[:], 0.0)
        bias_rows_f32 = const.tile([P, P], F32, name="bias_rows_f32")
        bias_cols = const.tile([P, P], F32, name="bias_cols")

        rows_by_entry = TILES * AGENTS
        mixes = TENSOR_TILES * UNITS
        rows = rows_by_entry + mixes
        raw = const.tile([P, rows * E], BF16, name="raw")
        comb = const.tile([P, rows * E], F32, name="comb")
        comb_top = const.tile([P, rows], F32, name="comb_top")
        comb_sum = const.tile([P, rows], F32, name="comb_sum")
        comb_by_agent = comb[:, rows_by_entry * E :]
        own_entry = const.tile([P, ENTRIES], F32, name="own_entry")
        spread = const.tile([P, mixes * E, ENTRIES], F32, name="spread")
        mix = const.tile([P, mixes, P], F32, name="mix")
        mix_ps_of = {}

        def load_logits_by_entry():
            nc.sync.dma_start(
                out=raw[:, 0 : rows_by_entry * E].rearrange("b (t c) -> b t c", t=TILES),
                in_=logits.rearrange("(t b) n e -> b t (n e)", b=P),
            )

        def load_bias_and_scales():
            nc.sync.dma_start(
                out=bias_rows[0 : E * L_BLOCKS, :], in_=b3.rearrange("e (c l) -> (e c) l", l=P)
            )
            for quadrant in range(4):
                nc.sync.dma_start(
                    out=w_scales[32 * quadrant : 32 * quadrant + 4].bitcast(I32),
                    in_=W3_scales.bitcast(I32)[:, 4 * quadrant : 4 * quadrant + 4, :].rearrange(
                        "e r n -> r e n"
                    ),
                )

        def load_words(pair):
            nc.sync.dma_start(
                out=w_words[:, 2 * pair : 2 * pair + 2, :].bitcast(I32),
                in_=W3_words.bitcast(I32)[2 * pair : 2 * pair + 2].rearrange("e p n -> p e n"),
            )

        def load_logits_by_agent():
            nc.sync.dma_start(
                out=raw[:, rows_by_entry * E :].rearrange("r (g e) -> r g e", e=E),
                in_=logits[(TILES - TENSOR_TILES) * P :].rearrange("(g b) n e -> (b n) g e", b=ENTRIES),
            )

        def widen_bias():
            nc.vector.tensor_copy(out=bias_rows_f32[:], in_=bias_rows[:])

        def turn_bias():
            bias_ps = psum_one.tile([P, P], F32, name="bias_ps", tag="o_ps")
            nc.tensor.transpose(bias_ps[:], bias_rows_f32[:], ident[:])
            mix_ps_of["bias"] = bias_ps

        def keep_bias():
            nc.scalar.copy(out=bias_cols[:], in_=mix_ps_of["bias"][:])

        def softmax_pieces(lo, hi):
            columns = slice(lo * E, hi * E)
            return [
                lambda: nc.vector.tensor_reduce(
                    out=comb_top[:, lo:hi], in_=by_group(raw[:, columns]), axis=AXIS_X, op=ALU.max
                ),
                lambda: nc.vector.tensor_tensor(
                    out=by_group(comb[:, columns]),
                    in0=by_group(raw[:, columns]),
                    in1=over_group(comb_top[:, lo:hi], hi - lo),
                    op=ALU.subtract,
                ),
                lambda: nc.scalar.activation(out=comb[:, columns], in_=comb[:, columns], func=ACT.Exp),
                lambda: nc.vector.tensor_reduce(
                    out=comb_sum[:, lo:hi], in_=by_group(comb[:, columns]), axis=AXIS_X, op=ALU.add
                ),
                lambda: nc.vector.reciprocal(out=comb_sum[:, lo:hi], in_=comb_sum[:, lo:hi]),
                lambda: nc.vector.tensor_tensor(
                    out=by_group(comb[:, columns]),
                    in0=by_group(comb[:, columns]),
                    in1=over_group(comb_sum[:, lo:hi], hi - lo),
                    op=ALU.mult,
                ),
            ]

        def mark_own_entry():
            nc.vector.tensor_reduce(
                out=own_entry[:],
                in_=ident[:].rearrange("p (b n) -> p b n", n=AGENTS),
                axis=AXIS_X,
                op=ALU.add,
            )

        def spread_out(first):
            shape = [P, 4 * E, ENTRIES]
            nc.gpsimd.tensor_tensor(
                out=spread[:, first * E : (first + 4) * E, :],
                in0=comb_by_agent[:, first * E : (first + 4) * E].unsqueeze(2).to_broadcast(shape),
                in1=own_entry[:].unsqueeze(1).to_broadcast(shape),
                op=ALU.mult,
            )

        def turn_mix(first):
            mix_ps = psum_one.tile([P, 4, P], F32, name="mix_ps", tag="o_ps")
            for i in range(4):
                unit_rows = spread[:, (first + i) * E : (first + i + 1) * E, :]
                nc.tensor.transpose(
                    mix_ps[:, i, :], unit_rows.rearrange("p e b -> p (e b)"), ident[:]
                )
            mix_ps_of[first] = mix_ps

        def keep_mix(first):
            nc.scalar.copy(out=mix[:, first : first + 4, :], in_=mix_ps_of[first][:])

        plan, turns = {}, {}

        def plan_at(step, piece):
            plan.setdefault(step, []).append(piece)

        plan_at(-TURN_H2, widen_bias)
        turns[-REGROUP] = [turn_bias]
        plan_at(-MULTIPLY, keep_bias)
        for step, piece in zip(AGENT_SOFTMAX, softmax_pieces(rows_by_entry, rows)):
            plan_at(step, piece)
        for step, piece in zip(ENTRY_SOFTMAX, softmax_pieces(0, rows_by_entry)):
            plan_at(step, piece)
        plan_at(-TURN_BACK, mark_own_entry)
        for i in range(mixes // 4):
            plan_at(SPREAD + i, lambda i=i: spread_out(4 * i))
            turns.setdefault(SPREAD + i + 1, []).append(lambda i=i: turn_mix(4 * i))
            plan_at(SPREAD + i + 2, lambda i=i: keep_mix(4 * i))

        x_of, grouped_of, codes_of, h_scales_of, zT_sb_of = {}, {}, {}, {}, {}
        xt_of, zT_of, z_ps_of, top_of, y_of, total_of, o_ps_of = {}, {}, {}, {}, {}, {}, {}
        terms_of, sumT_of, sumT_sb_of, factor_of, half_of = {}, {}, {}, {}, {}

        def load(t, pair):
            if pair == 0:
                x_sb = x_pool.tile([P, E * K], BF16, name="x_sb")
                x_of[t] = x_sb
            nc.sync.dma_start(
                out=x_of[t][:, 2 * pair * K : 2 * (pair + 1) * K],
                in_=h2[t * P : (t + 1) * P, 2 * pair : 2 * pair + 2, :].rearrange("b e k -> b (e k)"),
            )

        def turn_h2(t, pair):
            x_words = x_of[t][:].bitcast(F32)
            xt = psum_one.tile([P, 2, 2, P], F32, name="xt")
            for i in range(2):
                e = 2 * pair + i
                for u in range(2):
                    nc.tensor.transpose(
                        xt[:, i, u, :], x_words[:, e * WORDS + u : (e + 1) * WORDS : 2], ident[:]
                    )
            xt_of[t, pair] = xt

        def regroup(t, pair):
            if pair == 0:
                grouped = quant.tile([P, E * P * PACK], BF16, align_bytes=64, name="grouped")
                grouped_of[t] = grouped
            words = grouped_of[t][:].bitcast(F32).rearrange("p (e b u) -> p e b u", e=E, u=2)
            nc.scalar.copy(
                out=words[:, 2 * pair : 2 * pair + 2],
                in_=xt_of[t, pair][:].rearrange("p e u b -> p e b u"),
            )

        def quantise(t, pair):
            if pair == 0:
                codes = quant.tile([P, E * P], U32, align_bytes=64, name="codes")
                h_scales = quant.tile([P, E * P], U8, align_bytes=64, name="h_scales")
                codes_of[t] = codes
                h_scales_of[t] = h_scales
            columns = slice(2 * pair * P, 2 * (pair + 1) * P)
            nc.vector.quantize_mx(
                out=codes_of[t][:, columns].bitcast(FP8X4),
                scales=h_scales_of[t][:, columns],
                in_=grouped_of[t][:, 2 * pair * P * PACK : 2 * (pair + 1) * P * PACK],
            )

        def multiply(t, e):
            batch = slice(e * P, (e + 1) * P)
            zT = psum.tile([P, L_BLOCKS, P], F32, name="zT")
            for c in range(L_BLOCKS):
                nc.tensor.matmul_mx(
                    out=zT[:, c, :],
                    lhsT=w_words[:, e, 2 * c * P : 2 * (c + 1) * P].bitcast(FP4X4),
                    lhsT_scale=w_scales[:, e, c * P : (c + 1) * P],
                    rhs=codes_of[t][:, batch].bitcast(FP8X4),
                    rhs_scale=h_scales_of[t][:, batch],
                    start=True,
                    stop=True,
                )
            zT_of[t, e] = zT

        def add_bias(t, e):
            if e == 0:
                zT_sb = z_pool.tile([P, L_BLOCKS, UNITS, P], F32, name="zT_sb")
                zT_sb_of[t] = zT_sb
            for c in range(L_BLOCKS):
                if combines_on_tensor(t):
                    dst = zT_sb_of[t][:, c, :, e * ENTRIES : (e + 1) * ENTRIES]
                    src = zT_of[t, e][:, c, :].rearrange("p (g b) -> p g b", b=ENTRIES)
                else:
                    dst = zT_sb_of[t][:, c, e, :]
                    src = zT_of[t, e][:, c, :]
                column = e * L_BLOCKS + c
                nc.scalar.activation(
                    out=dst,
                    in_=src,
                    func=ACT.Identity,
                    bias=bias_cols[:, column : column + 1],
                    scale=1.0,
                )

        def turn_back(t, unit):
            z_ps = psum.tile([P, L], F32, name="z_ps")
            for c in range(L_BLOCKS):
                nc.tensor.transpose(
                    z_ps[:, c * P : (c + 1) * P], zT_sb_of[t][:, c, unit, :], ident[:]
                )
            z_ps_of[t, unit] = z_ps

        def find_top(t, unit):
            top = small.tile([P, GROUPS], F32, name="top")
            nc.vector.tensor_reduce(
                out=top[:], in_=by_group(z_ps_of[t, unit][:]), axis=AXIS_X, op=ALU.max
            )
            top_of[t, unit] = top

        def shift(t, unit):
            y = y_pool.tile([P, L], F32, name="y")
            nc.vector.tensor_tensor(
                out=by_group(y[:]),
                in0=by_group(z_ps_of[t, unit][:]),
                in1=over_group(top_of[t, unit][:], GROUPS),
                op=ALU.subtract,
            )
            y_of[t, unit] = y

        def exponent(t, unit):
            nc.scalar.activation(out=y_of[t, unit][:], in_=y_of[t, unit][:], func=ACT.Exp)

        def halve(t, unit):
            half = half_pool.tile([P, GROUPS, GROUP // 2], F32, name="half")
            eights = by_group(y_of[t, unit][:])
            nc.gpsimd.tensor_tensor(
                out=half[:], in0=eights[:, :, 0 : GROUP // 2], in1=eights[:, :, GROUP // 2 : GROUP], op=ALU.add
            )
            half_of[t, unit] = half

        def add_up(t, unit):
            total = small.tile([P, GROUPS], F32, name="total")
            nc.vector.tensor_reduce(out=total[:], in_=half_of[t, unit][:], axis=AXIS_X, op=ALU.add)
            total_of[t, unit] = total

        def invert(t, unit):
            factor = small.tile([P, GROUPS], F32, name="factor")
            nc.vector.reciprocal(out=factor[:], in_=total_of[t, unit][:])
            factor_of[t, unit] = factor

        def normalise(t, unit):
            nc.gpsimd.tensor_tensor(
                out=by_group(y_of[t, unit][:]),
                in0=by_group(y_of[t, unit][:]),
                in1=over_group(factor_of[t, unit][:], GROUPS),
                op=ALU.mult,
            )

        def combine_on_tensor(t, unit):
            o_ps = psum.tile([P, L], F32, name="o_ps", tag="sumT")
            nc.tensor.matmul(
                out=o_ps[:],
                lhsT=mix[:, mix_index(t, unit), :],
                rhs=y_of[t, unit][:],
                start=True,
                stop=True,
            )
            o_ps_of[t, unit] = o_ps

        def store_from_tensor(t, unit):
            o_sb = o_pool.tile([P, L], F32, name="o_sb")
            nc.scalar.copy(out=o_sb[:], in_=o_ps_of[t, unit][:])
            first_row = (t * P + unit * ENTRIES) * AGENTS
            nc.sync.dma_start(out=out_rows[first_row : first_row + P, :], in_=o_sb[:])

        def weight_of(t, n, e):
            column = (t * AGENTS + n) * E + e
            return comb[:, column : column + 1]

        def weigh(t, n, on_scalar):
            if (t, n) not in terms_of:
                terms_of[t, n] = {}
            for e in range(ADDED):
                if (e < scalar_terms(n)) != on_scalar:
                    continue
                weight = weight_of(t, n, e)
                term = term_pool.tile([P, L], F32, name="term")
                terms_of[t, n][e] = term
                if on_scalar:
                    nc.scalar.activation(out=term[:], in_=y_of[t, e][:], func=ACT.Copy, scale=weight)
                else:
                    nc.vector.tensor_scalar_mul(out=term[:], in0=y_of[t, e][:], scalar1=weight)

        def add_terms(t, n):
            sumT = psum.tile([P, L_BLOCKS, P], F32, name="sumT")
            for c in range(L_BLOCKS):
                for e in range(ADDED):
                    nc.tensor.matmul(
                        out=sumT[:, c, :],
                        lhsT=terms_of[t, n][e][:, c * P : (c + 1) * P],
                        rhs=ident[:],
                        is_transpose=True,
                        start=(e == 0),
                        stop=(e == ADDED - 1),
                    )
            sumT_of[t, n] = sumT

        def lift(t, n):
            sumT_sb = o_pool.tile([P, L_BLOCKS, P], F32, name="sumT_sb")
            nc.scalar.copy(out=sumT_sb[:], in_=sumT_of[t, n][:])
            sumT_sb_of[t, n] = sumT_sb

        def turn_out(t, n):
            o_ps = psum_one.tile([P, L], F32, name="o_ps")
            for c in range(L_BLOCKS):
                nc.tensor.transpose(o_ps[:, c * P : (c + 1) * P], sumT_sb_of[t, n][:, c, :], ident[:])
            o_ps_of[t, n] = o_ps

        def store_agent(t, n):
            o_sb = o_pool.tile([P, L], F32, name="o_sb")
            nc.vector.scalar_tensor_tensor(
                out=o_sb[:],
                in0=y_of[t, E - 1][:],
                scalar=weight_of(t, n, E - 1),
                in1=o_ps_of[t, n][:],
                op0=ALU.mult,
                op1=ALU.add,
            )
            nc.sync.dma_start(out=out[t * P : (t + 1) * P, n, :], in_=o_sb[:])

        def at(step, ahead):
            return divmod(step + ahead, UNITS)

        def real(t):
            return 0 <= t < TILES

        def gained(v):
            return min(FRONT_GAIN, max(0, (v - 4) // 2 + 1))

        def front(step, ahead):
            return [divmod(v, UNITS) for v in range(TOTAL_UNITS) if v - gained(v) - ahead == step]

        first_mixed = (TILES - TENSOR_TILES) * UNITS

        def mixed_at(v):
            steps, units = CATCH_UP
            return max(v - NORMALISE + 1, first_mixed + ((v - first_mixed) * steps + units - 1) // units)

        def mixed(step):
            return [divmod(v, UNITS) for v in range(first_mixed, TOTAL_UNITS) if mixed_at(v) == step]

        with tc.manual_schedule():
            for step in range(-LOAD, TOTAL_UNITS - STORE):
                for t, unit in front(step, ADD_BIAS):
                    add_bias(t, unit)
                t, unit = at(step, ADD_UP)
                if real(t):
                    halve(t, unit)
                t, unit = at(step, NORMALISE)
                if real(t):
                    invert(t, unit)
                    normalise(t, unit)
                t, unit = at(step, SHIFT)
                if real(t):
                    find_top(t, unit)
                t, unit = at(step, STORE)
                if real(t) and not combines_on_tensor(t):
                    store_agent(t, unit)
                t, unit = at(step, SHIFT)
                if real(t):
                    shift(t, unit)
                t, unit = at(step, ADD_UP)
                if real(t):
                    add_up(t, unit)
                for t, unit in mixed(step + LIFT):
                    store_from_tensor(t, unit)
                t, unit = at(step, LIFT)
                if real(t) and not combines_on_tensor(t):
                    lift(t, unit)
                t, unit = at(step, WEIGH)
                if real(t) and not combines_on_tensor(t):
                    weigh(t, unit, True)
                    weigh(t, unit, False)
                for t, unit in front(step, QUANTISE):
                    if unit % 2 == 0:
                        quantise(t, unit // 2)
                for piece in plan.get(step, []):
                    piece()
                for t, unit in front(step, REGROUP):
                    if unit % 2 == 0:
                        regroup(t, unit // 2)
                t, unit = at(step, EXPONENT)
                if real(t):
                    exponent(t, unit)
                t, unit = at(step, TURN_BACK)
                if real(t):
                    turn_back(t, unit)
                t, unit = at(step, COMBINE)
                if real(t) and not combines_on_tensor(t):
                    add_terms(t, unit)
                t, unit = at(step, TURN_OUT)
                if real(t) and not combines_on_tensor(t):
                    turn_out(t, unit)
                for piece in turns.get(step, []):
                    piece()
                for t, unit in front(step, MULTIPLY):
                    if unit % 2 == 0:
                        multiply(t, unit)
                        multiply(t, unit + 1)
                for t, unit in front(step, TURN_H2):
                    if unit % 2 == 0:
                        turn_h2(t, unit // 2)
                for t, unit in mixed(step):
                    combine_on_tensor(t, unit)
                for t, unit in front(step, LOAD):
                    if unit % 2 == 0:
                        load(t, unit // 2)
                        if t == 0:
                            if unit == 2:
                                load_bias_and_scales()
                                load_words(0)
                                load_logits_by_agent()
                                load_logits_by_entry()
                            if unit >= 4:
                                load_words(unit // 2 - 1)
                            if unit == 6:
                                load_words(3)
